import numpy as np
import ml_dtypes


def mxq(x, axis, fmt="e4m3"):
    dtype, down = {"e4m3": (ml_dtypes.float8_e4m3fn, 7), "e5m2": (ml_dtypes.float8_e5m2, 14)}[fmt]
    v = np.moveaxis(np.asarray(x, np.float32).astype(ml_dtypes.bfloat16).astype(np.float64), axis, -1)
    blocks = v.reshape(v.shape[:-1] + (-1, 32))
    amax = np.abs(blocks).max(-1, keepdims=True)
    byte = np.maximum(np.where(amax > 0, np.frexp(amax)[1] - 1 + 127, 0) - down, 1)
    scale = np.exp2(byte - 127.0)
    codes = (blocks / scale).astype(np.float32).astype(dtype).astype(np.float64)
    return np.moveaxis((codes * scale).reshape(v.shape), -1, axis)


WIDE = False


def mx_kscale(k):
    if not WIDE:
        return np.ones(k)
    levels = np.array([10, -10, 5, -5, 0])
    a = np.random.permutation(np.resize(levels, k // 512 * 4)).reshape(k // 512, 4)
    idx = np.arange(k)
    return np.exp2(a[idx // 512, idx % 128 // 32])


BF16 = ml_dtypes.bfloat16


def bf(x):
    return np.asarray(x, np.float32).astype(BF16)


def f64(x):
    return np.asarray(x).astype(np.float64)


B, L, C, K = 128, 8, 512, 5
F = C
BN_EPS = 1e-3
LEAKY_ALPHA = 0.3


def leaky(v):
    return np.where(v >= 0, v, LEAKY_ALPHA * v)


def bn(v, gamma, beta, mean, var):
    return gamma * (v - mean) * (1.0 / np.sqrt(var + BN_EPS)) + beta


def setup_inputs():
    s = mx_kscale(C)
    return {"x": bf(np.random.standard_normal((B, L, C)) * s),
            "k1": bf(np.random.standard_normal((K, L, C, F)) * 0.14 / np.sqrt(K * C) / s[:, None]),
            "b1": bf(np.random.standard_normal((L, F)) * 0.03),
            "gamma1": bf(1.0 + 0.1 * np.random.standard_normal(F)),
            "beta1": bf(np.random.standard_normal(F) * 0.2),
            "mean1": bf(np.random.standard_normal(F) * 0.05),
            "var1": bf(np.random.uniform(0.01, 0.03, F))}


def reference(x, k1, b1, gamma1, beta1, mean1, var1):
    xq = mxq(f64(x).transpose(1, 0, 2), 2, "e4m3")
    k = f64(k1)
    out = 2.0 * f64(b1)
    for i in range(k.shape[0]):
        step = (i // 2) * (-1 if i % 2 == 1 else 1)
        ki = np.roll(k[i], -step, axis=0) if step != 0 else k[i]
        p = xq @ mxq(ki, 1, "e4m3")
        p = np.roll(p, step, axis=0) if step != 0 else p
        out = out + p.transpose(1, 0, 2)
    return leaky(bn(out, f64(gamma1), f64(beta1), f64(mean1), f64(var1)))

@@ -1,0 +1,191 @@
+from contextlib import ExitStack
+
+import concourse.mybir as mybir
+from concourse.masks import make_identity
+
+F32 = mybir.dt.float32
+BF16 = mybir.dt.bfloat16
+U32 = mybir.dt.uint32
+U8 = mybir.dt.uint8
+FP8X4 = mybir.dt.float8_e4m3fn_x4
+ALU = mybir.AluOpType
+ACT = mybir.ActivationFunctionType
+
+P = 128
+PACK = 4
+B, L, C, TAPS = 128, 8, 512, 5
+F = C
+CHUNKS = F // P
+STEP = (0, 0, 1, -1, 2)
+BN_EPS = 1e-3
+ALPHA = 0.3
+NM = L * TAPS
+FLOPS = 2 * B * L * TAPS * C * F
+
+RAW_BUFS = 28
+N_SCALAR = 19
+
+
+def on_scalar(m):
+    return ((m + 1) * N_SCALAR) // NM > (m * N_SCALAR) // NM
+
+
+def tile_residualblock5_pa_kernel(tc, x, k1, b1, gamma1, beta1, mean1, var1, out):
+    nc = tc.nc
+    with ExitStack() as ctx:
+        const = ctx.enter_context(tc.tile_pool(name="const", bufs=1))
+        rawp = ctx.enter_context(tc.tile_pool(name="rawp", bufs=RAW_BUFS))
+        grpp = ctx.enter_context(tc.tile_pool(name="grpp", bufs=6))
+        codep = ctx.enter_context(tc.tile_pool(name="codep", bufs=8))
+        epip = ctx.enter_context(tc.tile_pool(name="epip", bufs=3))
+        psa = ctx.enter_context(tc.psum_pool(name="psa", bufs=1))
+        psm = ctx.enter_context(tc.psum_pool(name="psm", bufs=4))
+
+        raws, grps, codes, accs, vs, lvs, trs = {}, {}, {}, {}, {}, {}, {}
+
+        def load(m):
+            l, i = divmod(m, TAPS)
+            raw = rawp.tile([P, PACK, F], BF16, name="raw", tag="raw")
+            nc.sync.dma_start(out=raw[:], in_=k1[i, l, :, :].rearrange("(p j) f -> p j f", j=PACK))
+            raws[m] = raw
+
+        warm = const.tile([P, 1], F32, name="warm")
+        warm2 = const.tile([P, 1], F32, name="warm2")
+        nc.vector.memset(warm[:], 1.0)
+        nc.scalar.sqrt(out=warm2[:], in_=warm[:])
+        ident_f = const.tile([P, P], F32, name="ident_f")
+        make_identity(nc, ident_f[:])
+        ident_b = const.tile([P, P], BF16, name="ident_b")
+        make_identity(nc, ident_b[:])
+        vecs = const.tile([P, F], BF16, name="vecs")
+        nc.vector.memset(vecs[:], 0.0)
+
+        load(0)
+        load(1)
+        x_sb = const.tile([P, L * C], BF16, name="x_sb")
+        nc.sync.dma_start(out=x_sb[:], in_=x.rearrange("b l c -> b (l c)"))
+        nc.scalar.dma_start(out=vecs[0:L, :], in_=b1)
+        for r, vec in enumerate((gamma1, beta1, mean1, var1)):
+            nc.scalar.dma_start(out=vecs[L + r:L + r + 1, :], in_=vec.rearrange("(o f) -> o f", o=1))
+        for m in range(2, RAW_BUFS):
+            load(m)
+
+        gx = const.tile([P, L * B * PACK], BF16, name="gx", align_bytes=64)
+        xq = const.tile([P, L * B], U32, name="xq", align_bytes=64)
+        xs = const.tile([P, L * B], U8, name="xs", align_bytes=64)
+        s_t = const.tile([P, CHUNKS], F32, name="s_t")
+        t_t = const.tile([P, L, CHUNKS], F32, name="t_t")
+
+        def prep_x():
+            xv = x_sb[:].bitcast(F32).rearrange("b (l p u) -> b l u p", l=L, u=2)
+            gxw = gx[:].bitcast(F32).rearrange("p (l b u) -> p l b u", l=L, u=2)
+            for g in range(L // 2):
+                xt = psm.tile([P, 4, P], F32, name="xt", tag="m")
+                for dl in range(2):
+                    for u in range(2):
+                        nc.tensor.transpose(out=xt[:, 2 * dl + u, :], in_=xv[:, 2 * g + dl, u, :], identity=ident_f[:])
+                src = xt[:].rearrange("p (l u) b -> p l b u", u=2)
+                dst = gxw[:, 2 * g:2 * g + 2, :, :]
+                if g % 2 == 0:
+                    nc.vector.tensor_copy(out=dst, in_=src)
+                else:
+                    nc.scalar.copy(out=dst, in_=src)
+            nc.vector.quantize_mx(out=xq[:].bitcast(FP8X4), scales=xs[:], in_=gx[:])
+
+        def prep_bn():
+            vps = psm.tile([P, CHUNKS, P], BF16, name="vps", tag="m")
+            for c in range(CHUNKS):
+                nc.tensor.transpose(out=vps[:, c, :], in_=vecs[:, c * P:(c + 1) * P], identity=ident_b[:])
+            vt = const.tile([P, L + 4, CHUNKS], F32, name="vt")
+            nc.vector.tensor_copy(out=vt[:], in_=vps[:, :, 0:L + 4].rearrange("p c r -> p r c"))
+            varp = const.tile([P, CHUNKS], F32, name="varp")
+            nc.vector.tensor_scalar_add(out=varp[:], in0=vt[:, L + 3, :], scalar1=BN_EPS)
+            sd = const.tile([P, CHUNKS], F32, name="sd")
+            nc.scalar.sqrt(out=sd[:], in_=varp[:])
+            rs = const.tile([P, CHUNKS], F32, name="rs")
+            nc.vector.reciprocal(out=rs[:], in_=sd[:])
+            nc.vector.tensor_mul(out=s_t[:], in0=vt[:, L, :], in1=rs[:])
+            u1 = const.tile([P, L, CHUNKS], F32, name="u1")
+            nc.vector.scalar_tensor_tensor(
+                out=u1[:], in0=vt[:, 0:L, :], scalar=2.0,
+                in1=vt[:, L + 2:L + 3, :].to_broadcast([P, L, CHUNKS]),
+                op0=ALU.mult, op1=ALU.subtract)
+            u2 = const.tile([P, L, CHUNKS], F32, name="u2")
+            nc.vector.tensor_tensor(out=u2[:], in0=u1[:], in1=s_t[:].unsqueeze(1).to_broadcast([P, L, CHUNKS]), op=ALU.mult)
+            nc.vector.tensor_tensor(out=t_t[:], in0=u2[:], in1=vt[:, L + 1:L + 2, :].to_broadcast([P, L, CHUNKS]), op=ALU.add)
+
+        def regroup(m):
+            grp = grpp.tile([P, F, PACK], BF16, name="grp", tag="grp", align_bytes=64)
+            dst = grp[:].rearrange("p (c i) t -> p c t i", i=4)
+            src = raws[m][:].rearrange("p t (c i) -> p c t i", i=4)
+            if on_scalar(m):
+                nc.scalar.copy(out=dst, in_=src)
+            else:
+                nc.vector.tensor_copy(out=dst, in_=src)
+            grps[m] = grp
+
+        def quantise(m):
+            wq = codep.tile([P, F], U32, name="wq", tag="wq", align_bytes=64)
+            ws = codep.tile([P, F], U8, name="ws", tag="ws", align_bytes=64)
+            nc.vector.quantize_mx(out=wq[:].bitcast(FP8X4), scales=ws[:], in_=grps[m][:].rearrange("p f t -> p (f t)"))
+            codes[m] = (wq, ws)
+
+        def multiply(m):
+            l, i = divmod(m, TAPS)
+            if i == 0:
+                accs[l] = [psa.tile([P, B], F32, name="acc%d" % c, tag="acc%d" % c) for c in range(CHUNKS)]
+            wq, ws = codes[m]
+            pos = (l - STEP[i]) % L
+            for c in range(CHUNKS):
+                nc.tensor.matmul_mx(
+                    out=accs[l][c][:],
+                    lhsT=wq[:, c * P:(c + 1) * P].bitcast(FP8X4),
+                    lhsT_scale=ws[:, c * P:(c + 1) * P],
+                    rhs=xq[:, pos * B:(pos + 1) * B].bitcast(FP8X4),
+                    rhs_scale=xs[:, pos * B:(pos + 1) * B],
+                    start=(i == 0), stop=(i == TAPS - 1))
+
+        def affine(l):
+            v = epip.tile([P, CHUNKS * B], F32, name="v", tag="v")
+            for c in range(CHUNKS):
+                nc.scalar.activation(out=v[:, c * B:(c + 1) * B], in_=accs[l][c][:], func=ACT.Identity,
+                                     bias=t_t[:, l, c:c + 1], scale=s_t[:, c:c + 1])
+            vs[l] = v
+
+        def leaky(l):
+            lv = epip.tile([P, CHUNKS * B], F32, name="lv", tag="lv")
+            nc.vector.scalar_tensor_tensor(out=lv[:], in0=vs[l][:], scalar=ALPHA, in1=vs[l][:], op0=ALU.mult, op1=ALU.max)
+            lvs[l] = lv
+
+        def turn(l):
+            tr = psm.tile([P, F], F32, name="tr", tag="m")
+            for c in range(CHUNKS):
+                nc.tensor.transpose(out=tr[:, c * P:(c + 1) * P], in_=lvs[l][:, c * B:(c + 1) * B], identity=ident_f[:])
+            trs[l] = tr
+
+        def finish(l):
+            o = epip.tile([P, F], F32, name="o", tag="o")
+            nc.scalar.copy(out=o[:], in_=trs[l][:])
+            nc.scalar.dma_start(out=out[:, l, :], in_=o[:])
+
+        def at_end_of_position(m, fn):
+            if 0 <= m < NM and m % TAPS == TAPS - 1:
+                fn(m // TAPS)
+
+        for step in range(NM + 7):
+            if step < NM:
+                regroup(step)
+                if step + RAW_BUFS < NM:
+                    load(step + RAW_BUFS)
+            if step == 2:
+                prep_x()
+            if step == 4:
+                prep_bn()
+            if 0 <= step - 1 < NM:
+                quantise(step - 1)
+            if 0 <= step - 2 < NM:
+                multiply(step - 2)
+            at_end_of_position(step - 3, affine)
+            at_end_of_position(step - 4, leaky)
+            at_end_of_position(step - 5, turn)
+            at_end_of_position(step - 6, finish)

@@ -23,11 +23,9 @@ NM = L * TAPS
 FLOPS = 2 * B * L * TAPS * C * F
 
 RAW_BUFS = 28
-N_SCALAR = 19
-
-
-def on_scalar(m):
-    return ((m + 1) * N_SCALAR) // NM > (m * N_SCALAR) // NM
+LOAD_ORDER = (0, 1, 3, 2, 4)
+X_PIECES = (0, 6, 2, 4)
+SPLIT = 3 * P
 
 
 def tile_residualblock5_pa_kernel(tc, x, k1, b1, gamma1, beta1, mean1, var1, out):
@@ -40,68 +38,90 @@ def tile_residualblock5_pa_kernel(tc, x, k1, b1, gamma1, beta1, mean1, var1, out
         epip = ctx.enter_context(tc.tile_pool(name="epip", bufs=3))
         psa = ctx.enter_context(tc.psum_pool(name="psa", bufs=1))
         psm = ctx.enter_context(tc.psum_pool(name="psm", bufs=4))
+        ctx.enter_context(tc.manual_schedule())
 
+        seq = [(l, i) for l in range(L) for i in LOAD_ORDER]
+        state = {"next": 0}
         raws, grps, codes, accs, vs, lvs, trs = {}, {}, {}, {}, {}, {}, {}
+        x_raw, x_ps, x_grp = {}, {}, {}
 
-        def load(m):
-            l, i = divmod(m, TAPS)
-            raw = rawp.tile([P, PACK, F], BF16, name="raw", tag="raw")
-            nc.sync.dma_start(out=raw[:], in_=k1[i, l, :, :].rearrange("(p j) f -> p j f", j=PACK))
-            raws[m] = raw
+        def load_next():
+            if state["next"] < NM:
+                l, i = seq[state["next"]]
+                raw = rawp.tile([P, PACK, F], BF16, name="raw", tag="raw")
+                nc.sync.dma_start(out=raw[:], in_=k1[i, l, :, :].rearrange("(p j) f -> p j f", j=PACK))
+                raws[(l, i)] = raw
+                state["next"] = state["next"] + 1
 
+        def load_x(g):
+            xr = const.tile([P, 2 * C], BF16, name="xr%d" % g)
+            pa = X_PIECES[g]
+            nc.sync.dma_start(out=xr[:], in_=x[:, pa:pa + 2, :].rearrange("b l c -> b (l c)"))
+            x_raw[g] = xr
+
+        vecs = const.tile([P, F], BF16, name="vecs")
+        nc.gpsimd.memset(vecs[:], 0.0)
         warm = const.tile([P, 1], F32, name="warm")
         warm2 = const.tile([P, 1], F32, name="warm2")
-        nc.vector.memset(warm[:], 1.0)
+        nc.gpsimd.memset(warm[:], 1.0)
+        nc.scalar.dma_start(out=vecs[0:L, :], in_=b1)
+        for r, vec in enumerate((gamma1, beta1, mean1, var1)):
+            nc.scalar.dma_start(out=vecs[L + r:L + r + 1, :], in_=vec.rearrange("(o f) -> o f", o=1))
         nc.scalar.sqrt(out=warm2[:], in_=warm[:])
         ident_f = const.tile([P, P], F32, name="ident_f")
         make_identity(nc, ident_f[:])
         ident_b = const.tile([P, P], BF16, name="ident_b")
         make_identity(nc, ident_b[:])
-        vecs = const.tile([P, F], BF16, name="vecs")
-        nc.vector.memset(vecs[:], 0.0)
 
-        load(0)
-        load(1)
-        x_sb = const.tile([P, L * C], BF16, name="x_sb")
-        nc.sync.dma_start(out=x_sb[:], in_=x.rearrange("b l c -> b (l c)"))
-        nc.scalar.dma_start(out=vecs[0:L, :], in_=b1)
-        for r, vec in enumerate((gamma1, beta1, mean1, var1)):
-            nc.scalar.dma_start(out=vecs[L + r:L + r + 1, :], in_=vec.rearrange("(o f) -> o f", o=1))
-        for m in range(2, RAW_BUFS):
-            load(m)
+        for n in range(RAW_BUFS):
+            load_next()
+            if n == 2:
+                load_x(0)
+            if n == 3:
+                load_x(1)
+            if n == 4:
+                load_x(2)
+            if n == 9:
+                load_x(3)
 
-        gx = const.tile([P, L * B * PACK], BF16, name="gx", align_bytes=64)
         xq = const.tile([P, L * B], U32, name="xq", align_bytes=64)
         xs = const.tile([P, L * B], U8, name="xs", align_bytes=64)
         s_t = const.tile([P, CHUNKS], F32, name="s_t")
         t_t = const.tile([P, L, CHUNKS], F32, name="t_t")
+        vt = const.tile([P, L + 4, CHUNKS], F32, name="vt")
+        varp = const.tile([P, CHUNKS], F32, name="varp")
+        sd = const.tile([P, CHUNKS], F32, name="sd")
 
-        def prep_x():
-            xv = x_sb[:].bitcast(F32).rearrange("b (l p u) -> b l u p", l=L, u=2)
-            gxw = gx[:].bitcast(F32).rearrange("p (l b u) -> p l b u", l=L, u=2)
-            for g in range(L // 2):
-                xt = psm.tile([P, 4, P], F32, name="xt", tag="m")
-                for dl in range(2):
-                    for u in range(2):
-                        nc.tensor.transpose(out=xt[:, 2 * dl + u, :], in_=xv[:, 2 * g + dl, u, :], identity=ident_f[:])
-                src = xt[:].rearrange("p (l u) b -> p l b u", u=2)
-                dst = gxw[:, 2 * g:2 * g + 2, :, :]
-                if g % 2 == 0:
-                    nc.vector.tensor_copy(out=dst, in_=src)
-                else:
-                    nc.scalar.copy(out=dst, in_=src)
-            nc.vector.quantize_mx(out=xq[:].bitcast(FP8X4), scales=xs[:], in_=gx[:])
+        def x_turn(g):
+            xv = x_raw[g][:].bitcast(F32).rearrange("b (l p u) -> b l u p", l=2, u=2)
+            xt = psm.tile([P, 4, P], F32, name="xt", tag="m")
+            for dl in range(2):
+                for u in range(2):
+                    nc.tensor.transpose(out=xt[:, 2 * dl + u, :], in_=xv[:, dl, u, :], identity=ident_f[:])
+            x_ps[g] = xt
 
-        def prep_bn():
+        def x_exit(g, use_scalar):
+            gx = const.tile([P, 2 * B * PACK], BF16, name="gx%d" % g, align_bytes=64)
+            dst = gx[:].bitcast(F32).rearrange("p (l b u) -> p l b u", l=2, u=2)
+            src = x_ps[g][:].rearrange("p (l u) b -> p l b u", u=2)
+            if use_scalar:
+                nc.scalar.copy(out=dst, in_=src)
+            else:
+                nc.vector.tensor_copy(out=dst, in_=src)
+            x_grp[g] = gx
+
+        def x_quant(g):
+            cols = slice(X_PIECES[g] * B, (X_PIECES[g] + 2) * B)
+            nc.vector.quantize_mx(out=xq[:, cols].bitcast(FP8X4), scales=xs[:, cols], in_=x_grp[g][:])
+
+        def bn_part1():
             vps = psm.tile([P, CHUNKS, P], BF16, name="vps", tag="m")
             for c in range(CHUNKS):
                 nc.tensor.transpose(out=vps[:, c, :], in_=vecs[:, c * P:(c + 1) * P], identity=ident_b[:])
-            vt = const.tile([P, L + 4, CHUNKS], F32, name="vt")
             nc.vector.tensor_copy(out=vt[:], in_=vps[:, :, 0:L + 4].rearrange("p c r -> p r c"))
-            varp = const.tile([P, CHUNKS], F32, name="varp")
             nc.vector.tensor_scalar_add(out=varp[:], in0=vt[:, L + 3, :], scalar1=BN_EPS)
-            sd = const.tile([P, CHUNKS], F32, name="sd")
-            nc.scalar.sqrt(out=sd[:], in_=varp[:])
+
+        def bn_part2():
             rs = const.tile([P, CHUNKS], F32, name="rs")
             nc.vector.reciprocal(out=rs[:], in_=sd[:])
             nc.vector.tensor_mul(out=s_t[:], in0=vt[:, L, :], in1=rs[:])
@@ -114,78 +134,134 @@ def tile_residualblock5_pa_kernel(tc, x, k1, b1, gamma1, beta1, mean1, var1, out
             nc.vector.tensor_tensor(out=u2[:], in0=u1[:], in1=s_t[:].unsqueeze(1).to_broadcast([P, L, CHUNKS]), op=ALU.mult)
             nc.vector.tensor_tensor(out=t_t[:], in0=u2[:], in1=vt[:, L + 1:L + 2, :].to_broadcast([P, L, CHUNKS]), op=ALU.add)
 
-        def regroup(m):
-            grp = grpp.tile([P, F, PACK], BF16, name="grp", tag="grp", align_bytes=64)
-            dst = grp[:].rearrange("p (c i) t -> p c t i", i=4)
-            src = raws[m][:].rearrange("p t (c i) -> p c t i", i=4)
-            if on_scalar(m):
+        def regroup(l, i, use_scalar, f0, f1):
+            if (l, i) not in grps:
+                grps[(l, i)] = grpp.tile([P, F, PACK], BF16, name="grp", tag="grp", align_bytes=64)
+            dst = grps[(l, i)][:, f0:f1, :].rearrange("p (c i) t -> p c t i", i=4)
+            src = raws[(l, i)][:, :, f0:f1].rearrange("p t (c i) -> p c t i", i=4)
+            if use_scalar:
                 nc.scalar.copy(out=dst, in_=src)
             else:
                 nc.vector.tensor_copy(out=dst, in_=src)
-            grps[m] = grp
 
-        def quantise(m):
-            wq = codep.tile([P, F], U32, name="wq", tag="wq", align_bytes=64)
-            ws = codep.tile([P, F], U8, name="ws", tag="ws", align_bytes=64)
-            nc.vector.quantize_mx(out=wq[:].bitcast(FP8X4), scales=ws[:], in_=grps[m][:].rearrange("p f t -> p (f t)"))
-            codes[m] = (wq, ws)
+        def quantise(l, i, c0, c1):
+            if (l, i) not in codes:
+                wq = codep.tile([P, F], U32, name="wq", tag="wq", align_bytes=64)
+                ws = codep.tile([P, F], U8, name="ws", tag="ws", align_bytes=64)
+                codes[(l, i)] = (wq, ws)
+            wq, ws = codes[(l, i)]
+            cols = slice(c0 * P, c1 * P)
+            nc.vector.quantize_mx(out=wq[:, cols].bitcast(FP8X4), scales=ws[:, cols],
+                                  in_=grps[(l, i)][:, cols, :].rearrange("p f t -> p (f t)"))
 
-        def multiply(m):
-            l, i = divmod(m, TAPS)
-            if i == 0:
+        def multiply(l, i, c0, c1):
+            first = i == 0
+            if first:
                 accs[l] = [psa.tile([P, B], F32, name="acc%d" % c, tag="acc%d" % c) for c in range(CHUNKS)]
-            wq, ws = codes[m]
+            wq, ws = codes[(l, i)]
             pos = (l - STEP[i]) % L
-            for c in range(CHUNKS):
+            for c in range(c0, c1):
                 nc.tensor.matmul_mx(
                     out=accs[l][c][:],
                     lhsT=wq[:, c * P:(c + 1) * P].bitcast(FP8X4),
                     lhsT_scale=ws[:, c * P:(c + 1) * P],
                     rhs=xq[:, pos * B:(pos + 1) * B].bitcast(FP8X4),
                     rhs_scale=xs[:, pos * B:(pos + 1) * B],
-                    start=(i == 0), stop=(i == TAPS - 1))
+                    start=first, stop=(i == TAPS - 1))
 
-        def affine(l):
-            v = epip.tile([P, CHUNKS * B], F32, name="v", tag="v")
-            for c in range(CHUNKS):
-                nc.scalar.activation(out=v[:, c * B:(c + 1) * B], in_=accs[l][c][:], func=ACT.Identity,
+        def affine(l, c, use_scalar):
+            if l not in vs:
+                vs[l] = epip.tile([P, CHUNKS * B], F32, name="v", tag="v")
+            if use_scalar:
+                nc.scalar.activation(out=vs[l][:, c * B:(c + 1) * B], in_=accs[l][c][:], func=ACT.Identity,
                                      bias=t_t[:, l, c:c + 1], scale=s_t[:, c:c + 1])
-            vs[l] = v
+            else:
+                nc.vector.tensor_scalar(out=vs[l][:, c * B:(c + 1) * B], in0=accs[l][c][:],
+                                        scalar1=s_t[:, c:c + 1], scalar2=t_t[:, l, c:c + 1],
+                                        op0=ALU.mult, op1=ALU.add)
 
-        def leaky(l):
-            lv = epip.tile([P, CHUNKS * B], F32, name="lv", tag="lv")
-            nc.vector.scalar_tensor_tensor(out=lv[:], in0=vs[l][:], scalar=ALPHA, in1=vs[l][:], op0=ALU.mult, op1=ALU.max)
-            lvs[l] = lv
+        def leaky(l, c0, c1):
+            if l not in lvs:
+                lvs[l] = epip.tile([P, CHUNKS * B], F32, name="lv", tag="lv")
+            cols = slice(c0 * B, c1 * B)
+            nc.vector.scalar_tensor_tensor(out=lvs[l][:, cols], in0=vs[l][:, cols], scalar=ALPHA, in1=vs[l][:, cols],
+                                           op0=ALU.mult, op1=ALU.max)
 
-        def turn(l):
-            tr = psm.tile([P, F], F32, name="tr", tag="m")
-            for c in range(CHUNKS):
-                nc.tensor.transpose(out=tr[:, c * P:(c + 1) * P], in_=lvs[l][:, c * B:(c + 1) * B], identity=ident_f[:])
-            trs[l] = tr
+        def turn(l, c0, c1):
+            tr = psm.tile([P, (c1 - c0) * P], F32, name="tr", tag="m")
+            for c in range(c0, c1):
+                nc.tensor.transpose(out=tr[:, (c - c0) * P:(c - c0 + 1) * P], in_=lvs[l][:, c * B:(c + 1) * B], identity=ident_f[:])
+            trs[(l, c0)] = tr
 
-        def finish(l):
-            o = epip.tile([P, F], F32, name="o", tag="o")
-            nc.scalar.copy(out=o[:], in_=trs[l][:])
-            nc.scalar.dma_start(out=out[:, l, :], in_=o[:])
+        def finish(l, c0, c1, use_scalar):
+            o = epip.tile([P, (c1 - c0) * P], F32, name="o", tag="o%d" % c0)
+            if use_scalar:
+                nc.scalar.copy(out=o[:], in_=trs[(l, c0)][:])
+                nc.scalar.dma_start(out=out[:, l, c0 * P:c1 * P], in_=o[:])
+            else:
+                nc.vector.tensor_copy(out=o[:], in_=trs[(l, c0)][:])
+                nc.sync.dma_start(out=out[:, l, c0 * P:c1 * P], in_=o[:])
 
-        def at_end_of_position(m, fn):
-            if 0 <= m < NM and m % TAPS == TAPS - 1:
-                fn(m // TAPS)
+        for l in range(L):
+            regroup(l, 0, False, 0, F)
+            load_next()
+            regroup(l, 1, True, 0, F)
+            load_next()
+            if l >= 1:
+                quantise(l - 1, 4, 0, CHUNKS)
+                multiply(l - 1, 4, 0, CHUNKS)
+            regroup(l, 3, False, 0, F)
+            load_next()
+            if l == 0:
+                bn_part1()
+                x_turn(0)
+                x_exit(0, True)
+                nc.scalar.sqrt(out=sd[:], in_=varp[:])
+            else:
+                for c in range(CHUNKS):
+                    affine(l - 1, c, True)
+                if l <= 2:
+                    x_turn(l + 1)
+                    x_exit(l + 1, True)
+            quantise(l, 0, 0, CHUNKS)
+            if l == 0:
+                x_quant(0)
+            elif l <= 2:
+                x_quant(l + 1)
+            multiply(l, 0, 0, CHUNKS)
+            quantise(l, 1, 0, CHUNKS)
+            multiply(l, 1, 0, CHUNKS)
+            if l == 0:
+                bn_part2()
+            else:
+                leaky(l - 1, 0, CHUNKS)
+                turn(l - 1, 0, CHUNKS)
+            regroup(l, 2, True, 0, F)
+            load_next()
+            if l == 0:
+                x_turn(1)
+                x_exit(1, True)
+            if SPLIT < F:
+                regroup(l, 4, True, SPLIT, F)
+            if SPLIT > 0:
+                regroup(l, 4, False, 0, SPLIT)
+            load_next()
+            quantise(l, 3, 0, CHUNKS)
+            multiply(l, 3, 0, CHUNKS)
+            quantise(l, 2, 0, CHUNKS)
+            if l == 0:
+                x_quant(1)
+            multiply(l, 2, 0, CHUNKS)
+            if l >= 1:
+                finish(l - 1, 0, CHUNKS, True)
 
-        for step in range(NM + 7):
-            if step < NM:
-                regroup(step)
-                if step + RAW_BUFS < NM:
-                    load(step + RAW_BUFS)
-            if step == 2:
-                prep_x()
-            if step == 4:
-                prep_bn()
-            if 0 <= step - 1 < NM:
-                quantise(step - 1)
-            if 0 <= step - 2 < NM:
-                multiply(step - 2)
-            at_end_of_position(step - 3, affine)
-            at_end_of_position(step - 4, leaky)
-            at_end_of_position(step - 5, turn)
-            at_end_of_position(step - 6, finish)
+        last = L - 1
+        for c in range(CHUNKS):
+            quantise(last, 4, c, c + 1)
+            multiply(last, 4, c, c + 1)
+        for c in range(CHUNKS):
+            affine(last, c, True)
+            leaky(last, c, c + 1)
+            turn(last, c, c + 1)
+        for c in range(CHUNKS):
+            finish(last, c, c + 1, c % 2 == 0)

@@ -22,10 +22,13 @@ ALPHA = 0.3
 NM = L * TAPS
 FLOPS = 2 * B * L * TAPS * C * F
 
-RAW_BUFS = 28
+RAW_BUFS = 26
 LOAD_ORDER = (0, 1, 3, 2, 4)
 X_PIECES = (0, 6, 2, 4)
-SPLIT = 3 * P
+SPLIT = 448
+GROUP_OF = {0: ("a", 0), 1: ("a", 1), 3: ("b", 0), 2: ("b", 1), 4: ("c", 0)}
+GROUP_SIZE = {"a": 2, "b": 2, "c": 1}
+SUM_ON_PE = True
 
 
 def tile_residualblock5_pa_kernel(tc, x, k1, b1, gamma1, beta1, mean1, var1, out):
@@ -33,12 +36,11 @@ def tile_residualblock5_pa_kernel(tc, x, k1, b1, gamma1, beta1, mean1, var1, out
     with ExitStack() as ctx:
         const = ctx.enter_context(tc.tile_pool(name="const", bufs=1))
         rawp = ctx.enter_context(tc.tile_pool(name="rawp", bufs=RAW_BUFS))
-        grpp = ctx.enter_context(tc.tile_pool(name="grpp", bufs=6))
-        codep = ctx.enter_context(tc.tile_pool(name="codep", bufs=8))
+        grpp = ctx.enter_context(tc.tile_pool(name="grpp", bufs=2))
+        codep = ctx.enter_context(tc.tile_pool(name="codep", bufs=3))
         epip = ctx.enter_context(tc.tile_pool(name="epip", bufs=3))
         psa = ctx.enter_context(tc.psum_pool(name="psa", bufs=1))
         psm = ctx.enter_context(tc.psum_pool(name="psm", bufs=4))
-        ctx.enter_context(tc.manual_schedule())
 
         seq = [(l, i) for l in range(L) for i in LOAD_ORDER]
         state = {"next": 0}
@@ -49,7 +51,12 @@ def tile_residualblock5_pa_kernel(tc, x, k1, b1, gamma1, beta1, mean1, var1, out
             if state["next"] < NM:
                 l, i = seq[state["next"]]
                 raw = rawp.tile([P, PACK, F], BF16, name="raw", tag="raw")
-                nc.sync.dma_start(out=raw[:], in_=k1[i, l, :, :].rearrange("(p j) f -> p j f", j=PACK))
+                src = k1[i, l, :, :].rearrange("(p j) f -> p j f", j=PACK)
+                if state["next"] == 0:
+                    nc.sync.dma_start(out=raw[:, :, 0:F // 2], in_=src[:, :, 0:F // 2])
+                    nc.sync.dma_start(out=raw[:, :, F // 2:F], in_=src[:, :, F // 2:F])
+                else:
+                    nc.sync.dma_start(out=raw[:], in_=src)
                 raws[(l, i)] = raw
                 state["next"] = state["next"] + 1
 
@@ -100,14 +107,11 @@ def tile_residualblock5_pa_kernel(tc, x, k1, b1, gamma1, beta1, mean1, var1, out
                     nc.tensor.transpose(out=xt[:, 2 * dl + u, :], in_=xv[:, dl, u, :], identity=ident_f[:])
             x_ps[g] = xt
 
-        def x_exit(g, use_scalar):
+        def x_exit(g):
             gx = const.tile([P, 2 * B * PACK], BF16, name="gx%d" % g, align_bytes=64)
             dst = gx[:].bitcast(F32).rearrange("p (l b u) -> p l b u", l=2, u=2)
             src = x_ps[g][:].rearrange("p (l u) b -> p l b u", u=2)
-            if use_scalar:
-                nc.scalar.copy(out=dst, in_=src)
-            else:
-                nc.vector.tensor_copy(out=dst, in_=src)
+            nc.scalar.copy(out=dst, in_=src)
             x_grp[g] = gx
 
         def x_quant(g):
@@ -122,49 +126,57 @@ def tile_residualblock5_pa_kernel(tc, x, k1, b1, gamma1, beta1, mean1, var1, out
             nc.vector.tensor_scalar_add(out=varp[:], in0=vt[:, L + 3, :], scalar1=BN_EPS)
 
         def bn_part2():
+            pre = ALPHA if SUM_ON_PE else 1.0
             rs = const.tile([P, CHUNKS], F32, name="rs")
             nc.vector.reciprocal(out=rs[:], in_=sd[:])
-            nc.vector.tensor_mul(out=s_t[:], in0=vt[:, L, :], in1=rs[:])
+            s1 = const.tile([P, CHUNKS], F32, name="s1")
+            nc.vector.tensor_mul(out=s1[:], in0=vt[:, L, :], in1=rs[:])
             u1 = const.tile([P, L, CHUNKS], F32, name="u1")
             nc.vector.scalar_tensor_tensor(
                 out=u1[:], in0=vt[:, 0:L, :], scalar=2.0,
                 in1=vt[:, L + 2:L + 3, :].to_broadcast([P, L, CHUNKS]),
                 op0=ALU.mult, op1=ALU.subtract)
             u2 = const.tile([P, L, CHUNKS], F32, name="u2")
-            nc.vector.tensor_tensor(out=u2[:], in0=u1[:], in1=s_t[:].unsqueeze(1).to_broadcast([P, L, CHUNKS]), op=ALU.mult)
-            nc.vector.tensor_tensor(out=t_t[:], in0=u2[:], in1=vt[:, L + 1:L + 2, :].to_broadcast([P, L, CHUNKS]), op=ALU.add)
+            nc.vector.tensor_tensor(out=u2[:], in0=u1[:], in1=s1[:].unsqueeze(1).to_broadcast([P, L, CHUNKS]), op=ALU.mult)
+            u3 = const.tile([P, L, CHUNKS], F32, name="u3")
+            nc.vector.tensor_tensor(out=u3[:], in0=u2[:], in1=vt[:, L + 1:L + 2, :].to_broadcast([P, L, CHUNKS]), op=ALU.add)
+            nc.vector.tensor_scalar_mul(out=s_t[:], in0=s1[:], scalar1=pre)
+            nc.vector.tensor_scalar_mul(out=t_t[:], in0=u3[:], scalar1=pre)
 
         def regroup(l, i, use_scalar, f0, f1):
-            if (l, i) not in grps:
-                grps[(l, i)] = grpp.tile([P, F, PACK], BF16, name="grp", tag="grp", align_bytes=64)
-            dst = grps[(l, i)][:, f0:f1, :].rearrange("p (c i) t -> p c t i", i=4)
+            g, place = GROUP_OF[i]
+            if (l, g) not in grps:
+                grps[(l, g)] = grpp.tile([P, GROUP_SIZE[g], F, PACK], BF16, name="grp" + g, tag="grp" + g, align_bytes=64)
+            dst = grps[(l, g)][:, place, f0:f1, :].rearrange("p (c i) t -> p c t i", i=4)
             src = raws[(l, i)][:, :, f0:f1].rearrange("p t (c i) -> p c t i", i=4)
             if use_scalar:
                 nc.scalar.copy(out=dst, in_=src)
             else:
                 nc.vector.tensor_copy(out=dst, in_=src)
 
-        def quantise(l, i, c0, c1):
-            if (l, i) not in codes:
-                wq = codep.tile([P, F], U32, name="wq", tag="wq", align_bytes=64)
-                ws = codep.tile([P, F], U8, name="ws", tag="ws", align_bytes=64)
-                codes[(l, i)] = (wq, ws)
-            wq, ws = codes[(l, i)]
+        def quantise(l, g, c0, c1):
+            if (l, g) not in codes:
+                wq = codep.tile([P, GROUP_SIZE[g] * F], U32, name="wq" + g, tag="wq" + g, align_bytes=64)
+                ws = codep.tile([P, GROUP_SIZE[g] * F], U8, name="ws" + g, tag="ws" + g, align_bytes=64)
+                codes[(l, g)] = (wq, ws)
+            wq, ws = codes[(l, g)]
             cols = slice(c0 * P, c1 * P)
             nc.vector.quantize_mx(out=wq[:, cols].bitcast(FP8X4), scales=ws[:, cols],
-                                  in_=grps[(l, i)][:, cols, :].rearrange("p f t -> p (f t)"))
+                                  in_=grps[(l, g)][:].rearrange("p n f t -> p (n f) t")[:, cols, :].rearrange("p f t -> p (f t)"))
 
         def multiply(l, i, c0, c1):
             first = i == 0
             if first:
                 accs[l] = [psa.tile([P, B], F32, name="acc%d" % c, tag="acc%d" % c) for c in range(CHUNKS)]
-            wq, ws = codes[(l, i)]
+            g, place = GROUP_OF[i]
+            wq, ws = codes[(l, g)]
             pos = (l - STEP[i]) % L
             for c in range(c0, c1):
+                cols = slice(place * F + c * P, place * F + (c + 1) * P)
                 nc.tensor.matmul_mx(
                     out=accs[l][c][:],
-                    lhsT=wq[:, c * P:(c + 1) * P].bitcast(FP8X4),
-                    lhsT_scale=ws[:, c * P:(c + 1) * P],
+                    lhsT=wq[:, cols].bitcast(FP8X4),
+                    lhsT_scale=ws[:, cols],
                     rhs=xq[:, pos * B:(pos + 1) * B].bitcast(FP8X4),
                     rhs_scale=xs[:, pos * B:(pos + 1) * B],
                     start=first, stop=(i == TAPS - 1))
@@ -180,17 +192,28 @@ def tile_residualblock5_pa_kernel(tc, x, k1, b1, gamma1, beta1, mean1, var1, out
                                         scalar1=s_t[:, c:c + 1], scalar2=t_t[:, l, c:c + 1],
                                         op0=ALU.mult, op1=ALU.add)
 
-        def leaky(l, c0, c1):
+        def leaky(l, c0, c1, use_scalar):
             if l not in lvs:
                 lvs[l] = epip.tile([P, CHUNKS * B], F32, name="lv", tag="lv")
             cols = slice(c0 * B, c1 * B)
-            nc.vector.scalar_tensor_tensor(out=lvs[l][:, cols], in0=vs[l][:, cols], scalar=ALPHA, in1=vs[l][:, cols],
-                                           op0=ALU.mult, op1=ALU.max)
+            if not SUM_ON_PE:
+                nc.vector.scalar_tensor_tensor(out=lvs[l][:, cols], in0=vs[l][:, cols], scalar=ALPHA, in1=vs[l][:, cols],
+                                               op0=ALU.mult, op1=ALU.max)
+            elif use_scalar:
+                nc.scalar.activation(out=lvs[l][:, cols], in_=vs[l][:, cols], func=ACT.Relu, scale=(1.0 - ALPHA) / ALPHA)
+            else:
+                nc.vector.tensor_scalar(out=lvs[l][:, cols], in0=vs[l][:, cols], scalar1=(1.0 - ALPHA) / ALPHA, scalar2=0.0,
+                                        op0=ALU.mult, op1=ALU.max)
 
         def turn(l, c0, c1):
             tr = psm.tile([P, (c1 - c0) * P], F32, name="tr", tag="m")
             for c in range(c0, c1):
-                nc.tensor.transpose(out=tr[:, (c - c0) * P:(c - c0 + 1) * P], in_=lvs[l][:, c * B:(c + 1) * B], identity=ident_f[:])
+                dst = tr[:, (c - c0) * P:(c - c0 + 1) * P]
+                if SUM_ON_PE:
+                    nc.tensor.matmul(out=dst, lhsT=vs[l][:, c * B:(c + 1) * B], rhs=ident_f[:], is_transpose=True, start=True, stop=False)
+                    nc.tensor.matmul(out=dst, lhsT=lvs[l][:, c * B:(c + 1) * B], rhs=ident_f[:], is_transpose=True, start=False, stop=True)
+                else:
+                    nc.tensor.transpose(out=dst, in_=lvs[l][:, c * B:(c + 1) * B], identity=ident_f[:])
             trs[(l, c0)] = tr
 
         def finish(l, c0, c1, use_scalar):
@@ -203,65 +226,68 @@ def tile_residualblock5_pa_kernel(tc, x, k1, b1, gamma1, beta1, mean1, var1, out
                 nc.sync.dma_start(out=out[:, l, c0 * P:c1 * P], in_=o[:])
 
         for l in range(L):
-            regroup(l, 0, False, 0, F)
-            load_next()
-            regroup(l, 1, True, 0, F)
+            if l == 0:
+                regroup(l, 0, False, 0, F // 2)
+                regroup(l, 0, False, F // 2, F)
+            else:
+                regroup(l, 0, False, 0, F)
             load_next()
             if l >= 1:
-                quantise(l - 1, 4, 0, CHUNKS)
+                quantise(l - 1, "c", 0, CHUNKS)
                 multiply(l - 1, 4, 0, CHUNKS)
+            regroup(l, 1, True, 0, F)
+            load_next()
+            if l >= 2:
+                finish(l - 2, 0, CHUNKS, True)
             regroup(l, 3, False, 0, F)
             load_next()
             if l == 0:
                 bn_part1()
                 x_turn(0)
-                x_exit(0, True)
+                x_exit(0)
                 nc.scalar.sqrt(out=sd[:], in_=varp[:])
-            else:
+            elif l <= 2:
+                x_turn(l + 1)
+                x_exit(l + 1)
+            regroup(l, 2, True, 0, F)
+            load_next()
+            if l >= 1:
                 for c in range(CHUNKS):
                     affine(l - 1, c, True)
-                if l <= 2:
-                    x_turn(l + 1)
-                    x_exit(l + 1, True)
-            quantise(l, 0, 0, CHUNKS)
-            if l == 0:
-                x_quant(0)
-            elif l <= 2:
-                x_quant(l + 1)
+                if SUM_ON_PE:
+                    leaky(l - 1, 0, CHUNKS, True)
+                    turn(l - 1, 0, CHUNKS)
+            quantise(l, "a", 0, 2 * CHUNKS)
+            if l <= 2:
+                x_quant(0 if l == 0 else l + 1)
             multiply(l, 0, 0, CHUNKS)
-            quantise(l, 1, 0, CHUNKS)
             multiply(l, 1, 0, CHUNKS)
             if l == 0:
                 bn_part2()
-            else:
-                leaky(l - 1, 0, CHUNKS)
-                turn(l - 1, 0, CHUNKS)
-            regroup(l, 2, True, 0, F)
-            load_next()
-            if l == 0:
                 x_turn(1)
-                x_exit(1, True)
+                x_exit(1)
             if SPLIT < F:
                 regroup(l, 4, True, SPLIT, F)
             if SPLIT > 0:
                 regroup(l, 4, False, 0, SPLIT)
             load_next()
-            quantise(l, 3, 0, CHUNKS)
-            multiply(l, 3, 0, CHUNKS)
-            quantise(l, 2, 0, CHUNKS)
+            quantise(l, "b", 0, 2 * CHUNKS)
             if l == 0:
                 x_quant(1)
+            multiply(l, 3, 0, CHUNKS)
             multiply(l, 2, 0, CHUNKS)
-            if l >= 1:
-                finish(l - 1, 0, CHUNKS, True)
+            if l >= 1 and not SUM_ON_PE:
+                leaky(l - 1, 0, CHUNKS, False)
+                turn(l - 1, 0, CHUNKS)
 
         last = L - 1
         for c in range(CHUNKS):
-            quantise(last, 4, c, c + 1)
+            quantise(last, "c", c, c + 1)
             multiply(last, 4, c, c + 1)
+        finish(last - 1, 0, CHUNKS, True)
         for c in range(CHUNKS):
-            affine(last, c, True)
-            leaky(last, c, c + 1)
+            affine(last, c, c % 2 == 0)
+            leaky(last, c, c + 1, c % 2 == 0)
             turn(last, c, c + 1)
         for c in range(CHUNKS):
             finish(last, c, c + 1, c % 2 == 0)

@@ -22,10 +22,10 @@ ALPHA = 0.3
 NM = L * TAPS
 FLOPS = 2 * B * L * TAPS * C * F
 
-RAW_BUFS = 26
+RAW_BUFS = 24
 LOAD_ORDER = (0, 1, 3, 2, 4)
 X_PIECES = (0, 6, 2, 4)
-SPLIT = 448
+SPLIT = 416
 GROUP_OF = {0: ("a", 0), 1: ("a", 1), 3: ("b", 0), 2: ("b", 1), 4: ("c", 0)}
 GROUP_SIZE = {"a": 2, "b": 2, "c": 1}
 SUM_ON_PE = True
@@ -39,6 +39,7 @@ def tile_residualblock5_pa_kernel(tc, x, k1, b1, gamma1, beta1, mean1, var1, out
         grpp = ctx.enter_context(tc.tile_pool(name="grpp", bufs=2))
         codep = ctx.enter_context(tc.tile_pool(name="codep", bufs=3))
         epip = ctx.enter_context(tc.tile_pool(name="epip", bufs=3))
+        outp = ctx.enter_context(tc.tile_pool(name="outp", bufs=8))
         psa = ctx.enter_context(tc.psum_pool(name="psa", bufs=1))
         psm = ctx.enter_context(tc.psum_pool(name="psm", bufs=4))
 
@@ -127,21 +128,17 @@ def tile_residualblock5_pa_kernel(tc, x, k1, b1, gamma1, beta1, mean1, var1, out
 
         def bn_part2():
             pre = ALPHA if SUM_ON_PE else 1.0
+            wide = [P, L, CHUNKS]
             rs = const.tile([P, CHUNKS], F32, name="rs")
             nc.vector.reciprocal(out=rs[:], in_=sd[:])
-            s1 = const.tile([P, CHUNKS], F32, name="s1")
-            nc.vector.tensor_mul(out=s1[:], in0=vt[:, L, :], in1=rs[:])
-            u1 = const.tile([P, L, CHUNKS], F32, name="u1")
-            nc.vector.scalar_tensor_tensor(
-                out=u1[:], in0=vt[:, 0:L, :], scalar=2.0,
-                in1=vt[:, L + 2:L + 3, :].to_broadcast([P, L, CHUNKS]),
-                op0=ALU.mult, op1=ALU.subtract)
-            u2 = const.tile([P, L, CHUNKS], F32, name="u2")
-            nc.vector.tensor_tensor(out=u2[:], in0=u1[:], in1=s1[:].unsqueeze(1).to_broadcast([P, L, CHUNKS]), op=ALU.mult)
-            u3 = const.tile([P, L, CHUNKS], F32, name="u3")
-            nc.vector.tensor_tensor(out=u3[:], in0=u2[:], in1=vt[:, L + 1:L + 2, :].to_broadcast([P, L, CHUNKS]), op=ALU.add)
-            nc.vector.tensor_scalar_mul(out=s_t[:], in0=s1[:], scalar1=pre)
-            nc.vector.tensor_scalar_mul(out=t_t[:], in0=u3[:], scalar1=pre)
+            nc.vector.scalar_tensor_tensor(out=s_t[:], in0=vt[:, L, :], scalar=pre, in1=rs[:], op0=ALU.mult, op1=ALU.mult)
+            u1 = const.tile(wide, F32, name="u1")
+            nc.vector.scalar_tensor_tensor(out=u1[:], in0=vt[:, 0:L, :], scalar=2.0, in1=vt[:, L + 2:L + 3, :].to_broadcast(wide),
+                                           op0=ALU.mult, op1=ALU.subtract)
+            u2 = const.tile(wide, F32, name="u2")
+            nc.vector.tensor_tensor(out=u2[:], in0=u1[:], in1=s_t[:].unsqueeze(1).to_broadcast(wide), op=ALU.mult)
+            nc.vector.scalar_tensor_tensor(out=t_t[:], in0=vt[:, L + 1:L + 2, :].to_broadcast(wide), scalar=pre, in1=u2[:],
+                                           op0=ALU.mult, op1=ALU.add)
 
         def regroup(l, i, use_scalar, f0, f1):
             g, place = GROUP_OF[i]
@@ -217,6 +214,11 @@ def tile_residualblock5_pa_kernel(tc, x, k1, b1, gamma1, beta1, mean1, var1, out
             trs[(l, c0)] = tr
 
         def finish(l, c0, c1, use_scalar):
+            if c1 - c0 == CHUNKS:
+                o = outp.tile([P, F], F32, name="ofull", tag="ofull")
+                nc.scalar.copy(out=o[:], in_=trs[(l, c0)][:])
+                nc.gpsimd.dma_start(out=out[:, l, :], in_=o[:])
+                return
             o = epip.tile([P, (c1 - c0) * P], F32, name="o", tag="o%d" % c0)
             if use_scalar:
                 nc.scalar.copy(out=o[:], in_=trs[(l, c0)][:])
@@ -255,7 +257,7 @@ def tile_residualblock5_pa_kernel(tc, x, k1, b1, gamma1, beta1, mean1, var1, out
                 for c in range(CHUNKS):
                     affine(l - 1, c, True)
                 if SUM_ON_PE:
-                    leaky(l - 1, 0, CHUNKS, True)
+                    leaky(l - 1, 0, CHUNKS, False)
                     turn(l - 1, 0, CHUNKS)
             quantise(l, "a", 0, 2 * CHUNKS)
             if l <= 2:

@@ -26,6 +26,7 @@ RAW_BUFS = 24
 LOAD_ORDER = (0, 1, 3, 2, 4)
 X_PIECES = (0, 6, 2, 4)
 SPLIT = 416
+HOLD = 6
 GROUP_OF = {0: ("a", 0), 1: ("a", 1), 3: ("b", 0), 2: ("b", 1), 4: ("c", 0)}
 GROUP_SIZE = {"a": 2, "b": 2, "c": 1}
 SUM_ON_PE = True
@@ -39,7 +40,6 @@ def tile_residualblock5_pa_kernel(tc, x, k1, b1, gamma1, beta1, mean1, var1, out
         grpp = ctx.enter_context(tc.tile_pool(name="grpp", bufs=2))
         codep = ctx.enter_context(tc.tile_pool(name="codep", bufs=3))
         epip = ctx.enter_context(tc.tile_pool(name="epip", bufs=3))
-        outp = ctx.enter_context(tc.tile_pool(name="outp", bufs=8))
         psa = ctx.enter_context(tc.psum_pool(name="psa", bufs=1))
         psm = ctx.enter_context(tc.psum_pool(name="psm", bufs=4))
 
@@ -92,6 +92,7 @@ def tile_residualblock5_pa_kernel(tc, x, k1, b1, gamma1, beta1, mean1, var1, out
             if n == 9:
                 load_x(3)
 
+        o_all = const.tile([P, L, F], F32, name="o_all")
         xq = const.tile([P, L * B], U32, name="xq", align_bytes=64)
         xs = const.tile([P, L * B], U8, name="xs", align_bytes=64)
         s_t = const.tile([P, CHUNKS], F32, name="s_t")
@@ -214,18 +215,17 @@ def tile_residualblock5_pa_kernel(tc, x, k1, b1, gamma1, beta1, mean1, var1, out
             trs[(l, c0)] = tr
 
         def finish(l, c0, c1, use_scalar):
-            if c1 - c0 == CHUNKS:
-                o = outp.tile([P, F], F32, name="ofull", tag="ofull")
-                nc.scalar.copy(out=o[:], in_=trs[(l, c0)][:])
-                nc.gpsimd.dma_start(out=out[:, l, :], in_=o[:])
-                return
-            o = epip.tile([P, (c1 - c0) * P], F32, name="o", tag="o%d" % c0)
+            dst = o_all[:, l, c0 * P:c1 * P]
             if use_scalar:
-                nc.scalar.copy(out=o[:], in_=trs[(l, c0)][:])
-                nc.scalar.dma_start(out=out[:, l, c0 * P:c1 * P], in_=o[:])
+                nc.scalar.copy(out=dst, in_=trs[(l, c0)][:])
             else:
-                nc.vector.tensor_copy(out=o[:], in_=trs[(l, c0)][:])
-                nc.sync.dma_start(out=out[:, l, c0 * P:c1 * P], in_=o[:])
+                nc.vector.tensor_copy(out=dst, in_=trs[(l, c0)][:])
+            if l == HOLD - 1:
+                nc.sync.dma_start(out=out[:, 0:HOLD, :], in_=o_all[:, 0:HOLD, :])
+            elif l >= HOLD and use_scalar:
+                nc.scalar.dma_start(out=out[:, l, c0 * P:c1 * P], in_=dst)
+            elif l >= HOLD:
+                nc.sync.dma_start(out=out[:, l, c0 * P:c1 * P], in_=dst)
 
         for l in range(L):
             if l == 0:

@@ -25,9 +25,9 @@ FLOPS = 2 * B * L * TAPS * C * F
 RAW_BUFS = 24
 LOAD_ORDER = (0, 1, 3, 2, 4)
 X_PIECES = (0, 6, 2, 4)
-SPLIT = 416
+TAP4_V = (512, 512, 0, 512, 512, 0, 512, 256)
 HOLD = 6
-GROUP_OF = {0: ("a", 0), 1: ("a", 1), 3: ("b", 0), 2: ("b", 1), 4: ("c", 0)}
+GROUP_OF = {0: ("a", 0), 3: ("a", 1), 1: ("b", 0), 2: ("b", 1), 4: ("c", 0)}
 GROUP_SIZE = {"a": 2, "b": 2, "c": 1}
 SUM_ON_PE = True
 
@@ -263,20 +263,20 @@ def tile_residualblock5_pa_kernel(tc, x, k1, b1, gamma1, beta1, mean1, var1, out
             if l <= 2:
                 x_quant(0 if l == 0 else l + 1)
             multiply(l, 0, 0, CHUNKS)
-            multiply(l, 1, 0, CHUNKS)
+            multiply(l, 3, 0, CHUNKS)
             if l == 0:
                 bn_part2()
                 x_turn(1)
                 x_exit(1)
-            if SPLIT < F:
-                regroup(l, 4, True, SPLIT, F)
-            if SPLIT > 0:
-                regroup(l, 4, False, 0, SPLIT)
+            if TAP4_V[l] < F:
+                regroup(l, 4, True, TAP4_V[l], F)
+            if TAP4_V[l] > 0:
+                regroup(l, 4, False, 0, TAP4_V[l])
             load_next()
             quantise(l, "b", 0, 2 * CHUNKS)
             if l == 0:
                 x_quant(1)
-            multiply(l, 3, 0, CHUNKS)
+            multiply(l, 1, 0, CHUNKS)
             multiply(l, 2, 0, CHUNKS)
             if l >= 1 and not SUM_ON_PE:
                 leaky(l - 1, 0, CHUNKS, False)

@@ -234,15 +234,15 @@ def tile_residualblock5_pa_kernel(tc, x, k1, b1, gamma1, beta1, mean1, var1, out
             else:
                 regroup(l, 0, False, 0, F)
             load_next()
+            regroup(l, 1, True, 0, F)
+            load_next()
+            regroup(l, 3, False, 0, F)
+            load_next()
             if l >= 1:
                 quantise(l - 1, "c", 0, CHUNKS)
                 multiply(l - 1, 4, 0, CHUNKS)
-            regroup(l, 1, True, 0, F)
-            load_next()
             if l >= 2:
                 finish(l - 2, 0, CHUNKS, True)
-            regroup(l, 3, False, 0, F)
-            load_next()
             if l == 0:
                 bn_part1()
                 x_turn(0)

@@ -25,7 +25,7 @@ FLOPS = 2 * B * L * TAPS * C * F
 RAW_BUFS = 24
 LOAD_ORDER = (0, 1, 3, 2, 4)
 X_PIECES = (0, 6, 2, 4)
-TAP4_V = (512, 512, 0, 512, 512, 0, 512, 256)
+TAP4_V = (304, 304, 304, 304, 304, 304, 304, 304)
 HOLD = 6
 GROUP_OF = {0: ("a", 0), 3: ("a", 1), 1: ("b", 0), 2: ("b", 1), 4: ("c", 0)}
 GROUP_SIZE = {"a": 2, "b": 2, "c": 1}
@@ -46,7 +46,7 @@ def tile_residualblock5_pa_kernel(tc, x, k1, b1, gamma1, beta1, mean1, var1, out
         seq = [(l, i) for l in range(L) for i in LOAD_ORDER]
         state = {"next": 0}
         raws, grps, codes, accs, vs, lvs, trs = {}, {}, {}, {}, {}, {}, {}
-        x_raw, x_ps, x_grp = {}, {}, {}
+        x_raw, x_ps, x_grp, zps = {}, {}, {}, {}
 
         def load_next():
             if state["next"] < NM:
@@ -152,6 +152,25 @@ def tile_residualblock5_pa_kernel(tc, x, k1, b1, gamma1, beta1, mean1, var1, out
             else:
                 nc.vector.tensor_copy(out=dst, in_=src)
 
+        def pe_zip(l, i, h):
+            half = F // 2
+            zp = psm.tile([P, 2, half, 2], BF16, name="zp", tag="m")
+            zps[(l, i)] = zp
+            for u in range(2):
+                nc.tensor.matmul(out=zp[:, u, :, :].rearrange("p f e -> p (f e)"), lhsT=ident_b[:],
+                                 rhs=raws[(l, i)][:, 2 * u:2 * u + 2, h * half:(h + 1) * half].rearrange("p e f -> p f e"),
+                                 start=True, stop=True)
+
+        def zip_exit(l, i, h):
+            g, place = GROUP_OF[i]
+            if (l, g) not in grps:
+                grps[(l, g)] = grpp.tile([P, GROUP_SIZE[g], F, PACK], BF16, name="grp" + g, tag="grp" + g, align_bytes=64)
+            half = F // 2
+            zp = zps[(l, i)]
+            dst = grps[(l, g)][:, place, h * half:(h + 1) * half, :].rearrange("p f t -> p (f t)").bitcast(F32)
+            src = zp[:].rearrange("p u f e -> p (u f e)").bitcast(F32).rearrange("p (u f) -> p f u", u=2)
+            nc.scalar.copy(out=dst.rearrange("p (f u) -> p f u", u=2), in_=src)
+
         def quantise(l, g, c0, c1):
             if (l, g) not in codes:
                 wq = codep.tile([P, GROUP_SIZE[g] * F], U32, name="wq" + g, tag="wq" + g, align_bytes=64)
@@ -251,7 +270,12 @@ def tile_residualblock5_pa_kernel(tc, x, k1, b1, gamma1, beta1, mean1, var1, out
             elif l <= 2:
                 x_turn(l + 1)
                 x_exit(l + 1)
-            regroup(l, 2, True, 0, F)
+            if l == 0:
+                pe_zip(0, 2, 1)
+            zip_exit(l, 2, 1)
+            if l + 1 < L:
+                pe_zip(l + 1, 2, 1)
+            regroup(l, 2, True, 0, F // 2)
             load_next()
             if l >= 1:
                 for c in range(CHUNKS):

@@ -22,7 +22,9 @@ ALPHA = 0.3
 NM = L * TAPS
 FLOPS = 2 * B * L * TAPS * C * F
 
-RAW_BUFS = 24
+RAW_BUFS = 8
+PAIRED = (1, 2, 3, 4, 5, 6)
+X_AFTER = {2: 0, 3: 1, 4: 2, 7: 3}
 LOAD_ORDER = (0, 1, 3, 2, 4)
 X_PIECES = (0, 6, 2, 4)
 TAP4_V = (304, 304, 304, 304, 304, 304, 304, 304)
@@ -43,23 +45,46 @@ def tile_residualblock5_pa_kernel(tc, x, k1, b1, gamma1, beta1, mean1, var1, out
         psa = ctx.enter_context(tc.psum_pool(name="psa", bufs=1))
         psm = ctx.enter_context(tc.psum_pool(name="psm", bufs=4))
 
-        seq = [(l, i) for l in range(L) for i in LOAD_ORDER]
+        seq = []
+        for l in range(L):
+            if l in PAIRED:
+                seq.extend([(l, (0, 1)), (l, (2, 3)), (l, (4,))])
+            else:
+                seq.extend([(l, (i,)) for i in LOAD_ORDER])
         state = {"next": 0}
+        held = {"raw": [], "raw2": []}
+        done = set()
         raws, grps, codes, accs, vs, lvs, trs = {}, {}, {}, {}, {}, {}, {}
         x_raw, x_ps, x_grp, zps = {}, {}, {}, {}
 
-        def load_next():
-            if state["next"] < NM:
-                l, i = seq[state["next"]]
-                raw = rawp.tile([P, PACK, F], BF16, name="raw", tag="raw")
-                src = k1[i, l, :, :].rearrange("(p j) f -> p j f", j=PACK)
-                if state["next"] == 0:
-                    nc.sync.dma_start(out=raw[:, :, 0:F // 2], in_=src[:, :, 0:F // 2])
-                    nc.sync.dma_start(out=raw[:, :, F // 2:F], in_=src[:, :, F // 2:F])
+        def load_more(l_done, i_done):
+            done.add((l_done, i_done))
+            while state["next"] < len(seq):
+                n = state["next"]
+                l, taps = seq[n]
+                tag = "raw" if len(taps) == 1 else "raw2"
+                k = len(held[tag])
+                if k >= RAW_BUFS and not all(m in done for m in held[tag][k - RAW_BUFS]):
+                    return
+                held[tag].append([(l, i) for i in taps])
+                if len(taps) == 1:
+                    raw = rawp.tile([P, PACK, F], BF16, name="raw", tag="raw")
+                    src = k1[taps[0], l, :, :].rearrange("(p j) f -> p j f", j=PACK)
+                    if n == 0:
+                        nc.sync.dma_start(out=raw[:, :, 0:F // 2], in_=src[:, :, 0:F // 2])
+                        nc.sync.dma_start(out=raw[:, :, F // 2:F], in_=src[:, :, F // 2:F])
+                    else:
+                        nc.sync.dma_start(out=raw[:], in_=src)
+                    raws[(l, taps[0])] = raw[:]
                 else:
-                    nc.sync.dma_start(out=raw[:], in_=src)
-                raws[(l, i)] = raw
-                state["next"] = state["next"] + 1
+                    raw2 = rawp.tile([P, 2, PACK, F], BF16, name="raw2", tag="raw2")
+                    nc.sync.dma_start(out=raw2[:].rearrange("p i j f -> p i (j f)"),
+                                      in_=k1[taps[0]:taps[1] + 1, l, :, :].rearrange("i (p j) f -> p i (j f)", j=PACK))
+                    raws[(l, taps[0])] = raw2[:, 0, :, :]
+                    raws[(l, taps[1])] = raw2[:, 1, :, :]
+                state["next"] = n + 1
+                if n in X_AFTER:
+                    load_x(X_AFTER[n])
 
         def load_x(g):
             xr = const.tile([P, 2 * C], BF16, name="xr%d" % g)
@@ -81,16 +106,7 @@ def tile_residualblock5_pa_kernel(tc, x, k1, b1, gamma1, beta1, mean1, var1, out
         ident_b = const.tile([P, P], BF16, name="ident_b")
         make_identity(nc, ident_b[:])
 
-        for n in range(RAW_BUFS):
-            load_next()
-            if n == 2:
-                load_x(0)
-            if n == 3:
-                load_x(1)
-            if n == 4:
-                load_x(2)
-            if n == 9:
-                load_x(3)
+        load_more(-1, -1)
 
         o_all = const.tile([P, L, F], F32, name="o_all")
         xq = const.tile([P, L * B], U32, name="xq", align_bytes=64)
@@ -252,11 +268,11 @@ def tile_residualblock5_pa_kernel(tc, x, k1, b1, gamma1, beta1, mean1, var1, out
                 regroup(l, 0, False, F // 2, F)
             else:
                 regroup(l, 0, False, 0, F)
-            load_next()
+            load_more(l, 0)
             regroup(l, 1, True, 0, F)
-            load_next()
+            load_more(l, 1)
             regroup(l, 3, False, 0, F)
-            load_next()
+            load_more(l, 3)
             if l >= 1:
                 quantise(l - 1, "c", 0, CHUNKS)
                 multiply(l - 1, 4, 0, CHUNKS)
@@ -276,7 +292,7 @@ def tile_residualblock5_pa_kernel(tc, x, k1, b1, gamma1, beta1, mean1, var1, out
             if l + 1 < L:
                 pe_zip(l + 1, 2, 1)
             regroup(l, 2, True, 0, F // 2)
-            load_next()
+            load_more(l, 2)
             if l >= 1:
                 for c in range(CHUNKS):
                     affine(l - 1, c, True)
@@ -296,7 +312,7 @@ def tile_residualblock5_pa_kernel(tc, x, k1, b1, gamma1, beta1, mean1, var1, out
                 regroup(l, 4, True, TAP4_V[l], F)
             if TAP4_V[l] > 0:
                 regroup(l, 4, False, 0, TAP4_V[l])
-            load_next()
+            load_more(l, 4)
             quantise(l, "b", 0, 2 * CHUNKS)
             if l == 0:
                 x_quant(1)

@@ -262,7 +262,7 @@ def tile_residualblock5_pa_kernel(tc, x, k1, b1, gamma1, beta1, mean1, var1, out
             elif l >= HOLD:
                 nc.sync.dma_start(out=out[:, l, c0 * P:c1 * P], in_=dst)
 
-        for l in range(L):
+        for l in range(L - 1):
             if l == 0:
                 regroup(l, 0, False, 0, F // 2)
                 regroup(l, 0, False, F // 2, F)
@@ -323,6 +323,27 @@ def tile_residualblock5_pa_kernel(tc, x, k1, b1, gamma1, beta1, mean1, var1, out
                 turn(l - 1, 0, CHUNKS)
 
         last = L - 1
+        regroup(last, 0, False, 0, F)
+        regroup(last, 1, True, 0, F)
+        regroup(last, 3, False, 0, F)
+        quantise(last - 1, "c", 0, CHUNKS)
+        multiply(last - 1, 4, 0, CHUNKS)
+        finish(last - 2, 0, CHUNKS, True)
+        zip_exit(last, 2, 1)
+        regroup(last, 2, False, 0, F // 2)
+        for c in range(CHUNKS):
+            affine(last - 1, c, True)
+        leaky(last - 1, 0, CHUNKS, False)
+        turn(last - 1, 0, CHUNKS)
+        quantise(last, "a", 0, 2 * CHUNKS)
+        multiply(last, 0, 0, CHUNKS)
+        multiply(last, 3, 0, CHUNKS)
+        quantise(last, "b", 0, CHUNKS)
+        multiply(last, 1, 0, CHUNKS)
+        quantise(last, "b", CHUNKS, 2 * CHUNKS)
+        multiply(last, 2, 0, CHUNKS)
+        for c in range(CHUNKS):
+            regroup(last, 4, c % 2 == 1, c * P, (c + 1) * P)
         for c in range(CHUNKS):
             quantise(last, "c", c, c + 1)
             multiply(last, 4, c, c + 1)

@@ -24,7 +24,7 @@ FLOPS = 2 * B * L * TAPS * C * F
 
 RAW_BUFS = 8
 PAIRED = (1, 2, 3, 4, 5, 6)
-X_AFTER = {2: 0, 3: 1, 4: 2, 7: 3}
+X_AFTER = {2: 0, 3: 1}
 LOAD_ORDER = (0, 1, 3, 2, 4)
 X_PIECES = (0, 6, 2, 4)
 TAP4_V = (304, 304, 304, 304, 304, 304, 304, 304)
@@ -70,11 +70,7 @@ def tile_residualblock5_pa_kernel(tc, x, k1, b1, gamma1, beta1, mean1, var1, out
                 if len(taps) == 1:
                     raw = rawp.tile([P, PACK, F], BF16, name="raw", tag="raw")
                     src = k1[taps[0], l, :, :].rearrange("(p j) f -> p j f", j=PACK)
-                    if n == 0:
-                        nc.sync.dma_start(out=raw[:, :, 0:F // 2], in_=src[:, :, 0:F // 2])
-                        nc.sync.dma_start(out=raw[:, :, F // 2:F], in_=src[:, :, F // 2:F])
-                    else:
-                        nc.sync.dma_start(out=raw[:], in_=src)
+                    nc.sync.dma_start(out=raw[:], in_=src)
                     raws[(l, taps[0])] = raw[:]
                 else:
                     raw2 = rawp.tile([P, 2, PACK, F], BF16, name="raw2", tag="raw2")
@@ -86,11 +82,12 @@ def tile_residualblock5_pa_kernel(tc, x, k1, b1, gamma1, beta1, mean1, var1, out
                 if n in X_AFTER:
                     load_x(X_AFTER[n])
 
-        def load_x(g):
-            xr = const.tile([P, 2 * C], BF16, name="xr%d" % g)
-            pa = X_PIECES[g]
-            nc.sync.dma_start(out=xr[:], in_=x[:, pa:pa + 2, :].rearrange("b l c -> b (l c)"))
-            x_raw[g] = xr
+        def load_x(h):
+            xr = const.tile([P, 4 * C], BF16, name="xr%d" % h)
+            nc.sync.dma_start(out=xr[:], in_=x[:, 4 * h:4 * h + 4, :].rearrange("b l c -> b (l c)"))
+            for g, pa in enumerate(X_PIECES):
+                if pa // 4 == h:
+                    x_raw[g] = xr[:, (pa % 4) * C:(pa % 4 + 2) * C]
 
         vecs = const.tile([P, F], BF16, name="vecs")
         nc.gpsimd.memset(vecs[:], 0.0)
@@ -118,7 +115,7 @@ def tile_residualblock5_pa_kernel(tc, x, k1, b1, gamma1, beta1, mean1, var1, out
         sd = const.tile([P, CHUNKS], F32, name="sd")
 
         def x_turn(g):
-            xv = x_raw[g][:].bitcast(F32).rearrange("b (l p u) -> b l u p", l=2, u=2)
+            xv = x_raw[g].bitcast(F32).rearrange("b (l p u) -> b l u p", l=2, u=2)
             xt = psm.tile([P, 4, P], F32, name="xt", tag="m")
             for dl in range(2):
                 for u in range(2):
@@ -257,17 +254,11 @@ def tile_residualblock5_pa_kernel(tc, x, k1, b1, gamma1, beta1, mean1, var1, out
                 nc.vector.tensor_copy(out=dst, in_=trs[(l, c0)][:])
             if l == HOLD - 1:
                 nc.sync.dma_start(out=out[:, 0:HOLD, :], in_=o_all[:, 0:HOLD, :])
-            elif l >= HOLD and use_scalar:
-                nc.scalar.dma_start(out=out[:, l, c0 * P:c1 * P], in_=dst)
-            elif l >= HOLD:
-                nc.sync.dma_start(out=out[:, l, c0 * P:c1 * P], in_=dst)
+            elif l == HOLD:
+                nc.scalar.dma_start(out=out[:, l, :], in_=o_all[:, l, :])
 
         for l in range(L - 1):
-            if l == 0:
-                regroup(l, 0, False, 0, F // 2)
-                regroup(l, 0, False, F // 2, F)
-            else:
-                regroup(l, 0, False, 0, F)
+            regroup(l, 0, False, 0, F)
             load_more(l, 0)
             regroup(l, 1, True, 0, F)
             load_more(l, 1)
@@ -354,3 +345,4 @@ def tile_residualblock5_pa_kernel(tc, x, k1, b1, gamma1, beta1, mean1, var1, out
             turn(last, c, c + 1)
         for c in range(CHUNKS):
             finish(last, c, c + 1, c % 2 == 0)
+        nc.sync.dma_start(out=out[:, last, :], in_=o_all[:, last, :])

@@ -68,12 +68,12 @@ def tile_residualblock5_pa_kernel(tc, x, k1, b1, gamma1, beta1, mean1, var1, out
                     return
                 held[tag].append([(l, i) for i in taps])
                 if len(taps) == 1:
-                    raw = rawp.tile([P, PACK, F], BF16, name="raw", tag="raw")
+                    raw = rawp.tile([P, PACK, F], BF16, name="raw", tag="raw", align_bytes=256)
                     src = k1[taps[0], l, :, :].rearrange("(p j) f -> p j f", j=PACK)
                     nc.sync.dma_start(out=raw[:], in_=src)
                     raws[(l, taps[0])] = raw[:]
                 else:
-                    raw2 = rawp.tile([P, 2, PACK, F], BF16, name="raw2", tag="raw2")
+                    raw2 = rawp.tile([P, 2, PACK, F], BF16, name="raw2", tag="raw2", align_bytes=256)
                     nc.sync.dma_start(out=raw2[:].rearrange("p i j f -> p i (j f)"),
                                       in_=k1[taps[0]:taps[1] + 1, l, :, :].rearrange("i (p j) f -> p i (j f)", j=PACK))
                     raws[(l, taps[0])] = raw2[:, 0, :, :]
@@ -83,7 +83,7 @@ def tile_residualblock5_pa_kernel(tc, x, k1, b1, gamma1, beta1, mean1, var1, out
                     load_x(X_AFTER[n])
 
         def load_x(h):
-            xr = const.tile([P, 4 * C], BF16, name="xr%d" % h)
+            xr = const.tile([P, 4 * C], BF16, name="xr%d" % h, align_bytes=256)
             nc.sync.dma_start(out=xr[:], in_=x[:, 4 * h:4 * h + 4, :].rearrange("b l c -> b (l c)"))
             for g, pa in enumerate(X_PIECES):
                 if pa // 4 == h:
@@ -105,7 +105,7 @@ def tile_residualblock5_pa_kernel(tc, x, k1, b1, gamma1, beta1, mean1, var1, out
 
         load_more(-1, -1)
 
-        o_all = const.tile([P, L, F], F32, name="o_all")
+        o_all = const.tile([P, L, F], F32, name="o_all", align_bytes=256)
         xq = const.tile([P, L * B], U32, name="xq", align_bytes=64)
         xs = const.tile([P, L * B], U8, name="xs", align_bytes=64)
         s_t = const.tile([P, CHUNKS], F32, name="s_t")

@@ -29,6 +29,7 @@ LOAD_ORDER = (0, 1, 3, 2, 4)
 X_PIECES = (0, 6, 2, 4)
 TAP4_V = (304, 304, 304, 304, 304, 304, 304, 304)
 HOLD = 6
+RUN = 8
 GROUP_OF = {0: ("a", 0), 3: ("a", 1), 1: ("b", 0), 2: ("b", 1), 4: ("c", 0)}
 GROUP_SIZE = {"a": 2, "b": 2, "c": 1}
 SUM_ON_PE = True
@@ -158,8 +159,8 @@ def tile_residualblock5_pa_kernel(tc, x, k1, b1, gamma1, beta1, mean1, var1, out
             g, place = GROUP_OF[i]
             if (l, g) not in grps:
                 grps[(l, g)] = grpp.tile([P, GROUP_SIZE[g], F, PACK], BF16, name="grp" + g, tag="grp" + g, align_bytes=64)
-            dst = grps[(l, g)][:, place, f0:f1, :].rearrange("p (c i) t -> p c t i", i=4)
-            src = raws[(l, i)][:, :, f0:f1].rearrange("p t (c i) -> p c t i", i=4)
+            dst = grps[(l, g)][:, place, f0:f1, :].rearrange("p (c i) t -> p c t i", i=RUN)
+            src = raws[(l, i)][:, :, f0:f1].rearrange("p t (c i) -> p c t i", i=RUN)
             if use_scalar:
                 nc.scalar.copy(out=dst, in_=src)
             else:

@@ -27,7 +27,7 @@ PAIRED = (1, 2, 3, 4, 5, 6)
 X_AFTER = {2: 0, 3: 1}
 LOAD_ORDER = (0, 1, 3, 2, 4)
 X_PIECES = (0, 6, 2, 4)
-TAP4_V = (304, 304, 304, 304, 304, 304, 304, 304)
+TAP4_V = (416, 416, 416, 416, 416, 416, 416, 416)
 HOLD = 6
 RUN = 8
 GROUP_OF = {0: ("a", 0), 3: ("a", 1), 1: ("b", 0), 2: ("b", 1), 4: ("c", 0)}
@@ -98,7 +98,7 @@ def tile_residualblock5_pa_kernel(tc, x, k1, b1, gamma1, beta1, mean1, var1, out
         nc.scalar.dma_start(out=vecs[0:L, :], in_=b1)
         for r, vec in enumerate((gamma1, beta1, mean1, var1)):
             nc.scalar.dma_start(out=vecs[L + r:L + r + 1, :], in_=vec.rearrange("(o f) -> o f", o=1))
-        nc.scalar.sqrt(out=warm2[:], in_=warm[:])
+        nc.scalar.activation(out=warm2[:], in_=warm[:], func=ACT.Abs_reciprocal_sqrt)
         ident_f = const.tile([P, P], F32, name="ident_f")
         make_identity(nc, ident_f[:])
         ident_b = const.tile([P, P], BF16, name="ident_b")
@@ -112,8 +112,9 @@ def tile_residualblock5_pa_kernel(tc, x, k1, b1, gamma1, beta1, mean1, var1, out
         s_t = const.tile([P, CHUNKS], F32, name="s_t")
         t_t = const.tile([P, L, CHUNKS], F32, name="t_t")
         vt = const.tile([P, L + 4, CHUNKS], F32, name="vt")
-        varp = const.tile([P, CHUNKS], F32, name="varp")
-        sd = const.tile([P, CHUNKS], F32, name="sd")
+        rs = const.tile([P, CHUNKS], F32, name="rs")
+        eps = const.tile([P, 1], F32, name="eps")
+        nc.gpsimd.tensor_scalar(out=eps[:], in0=warm[:], scalar1=BN_EPS, scalar2=None, op0=ALU.mult)
 
         def x_turn(g):
             xv = x_raw[g].bitcast(F32).rearrange("b (l p u) -> b l u p", l=2, u=2)
@@ -139,13 +140,10 @@ def tile_residualblock5_pa_kernel(tc, x, k1, b1, gamma1, beta1, mean1, var1, out
             for c in range(CHUNKS):
                 nc.tensor.transpose(out=vps[:, c, :], in_=vecs[:, c * P:(c + 1) * P], identity=ident_b[:])
             nc.vector.tensor_copy(out=vt[:], in_=vps[:, :, 0:L + 4].rearrange("p c r -> p r c"))
-            nc.vector.tensor_scalar_add(out=varp[:], in0=vt[:, L + 3, :], scalar1=BN_EPS)
 
         def bn_part2():
             pre = ALPHA if SUM_ON_PE else 1.0
             wide = [P, L, CHUNKS]
-            rs = const.tile([P, CHUNKS], F32, name="rs")
-            nc.vector.reciprocal(out=rs[:], in_=sd[:])
             nc.vector.scalar_tensor_tensor(out=s_t[:], in0=vt[:, L, :], scalar=pre, in1=rs[:], op0=ALU.mult, op1=ALU.mult)
             u1 = const.tile(wide, F32, name="u1")
             nc.vector.scalar_tensor_tensor(out=u1[:], in0=vt[:, 0:L, :], scalar=2.0, in1=vt[:, L + 2:L + 3, :].to_broadcast(wide),
@@ -274,7 +272,7 @@ def tile_residualblock5_pa_kernel(tc, x, k1, b1, gamma1, beta1, mean1, var1, out
                 bn_part1()
                 x_turn(0)
                 x_exit(0)
-                nc.scalar.sqrt(out=sd[:], in_=varp[:])
+                nc.scalar.activation(out=rs[:], in_=vt[:, L + 3, :], func=ACT.Abs_reciprocal_sqrt, bias=eps[:])
             elif l <= 2:
                 x_turn(l + 1)
                 x_exit(l + 1)
@@ -289,7 +287,7 @@ def tile_residualblock5_pa_kernel(tc, x, k1, b1, gamma1, beta1, mean1, var1, out
                 for c in range(CHUNKS):
                     affine(l - 1, c, True)
                 if SUM_ON_PE:
-                    leaky(l - 1, 0, CHUNKS, False)
+                    leaky(l - 1, 0, CHUNKS, True)
                     turn(l - 1, 0, CHUNKS)
             quantise(l, "a", 0, 2 * CHUNKS)
             if l <= 2:
@@ -325,7 +323,7 @@ def tile_residualblock5_pa_kernel(tc, x, k1, b1, gamma1, beta1, mean1, var1, out
         regroup(last, 2, False, 0, F // 2)
         for c in range(CHUNKS):
             affine(last - 1, c, True)
-        leaky(last - 1, 0, CHUNKS, False)
+        leaky(last - 1, 0, CHUNKS, True)
         turn(last - 1, 0, CHUNKS)
         quantise(last, "a", 0, 2 * CHUNKS)
         multiply(last, 0, 0, CHUNKS)

@@ -28,7 +28,7 @@ X_AFTER = {2: 0, 3: 1}
 LOAD_ORDER = (0, 1, 3, 2, 4)
 X_PIECES = (0, 6, 2, 4)
 TAP4_V = (416, 416, 416, 416, 416, 416, 416, 416)
-HOLD = 6
+HOLD = 5
 RUN = 8
 GROUP_OF = {0: ("a", 0), 3: ("a", 1), 1: ("b", 0), 2: ("b", 1), 4: ("c", 0)}
 GROUP_SIZE = {"a": 2, "b": 2, "c": 1}
@@ -253,8 +253,8 @@ def tile_residualblock5_pa_kernel(tc, x, k1, b1, gamma1, beta1, mean1, var1, out
                 nc.vector.tensor_copy(out=dst, in_=trs[(l, c0)][:])
             if l == HOLD - 1:
                 nc.sync.dma_start(out=out[:, 0:HOLD, :], in_=o_all[:, 0:HOLD, :])
-            elif l == HOLD:
-                nc.scalar.dma_start(out=out[:, l, :], in_=o_all[:, l, :])
+            elif HOLD <= l < L - 1:
+                nc.sync.dma_start(out=out[:, l, :], in_=o_all[:, l, :])
 
         for l in range(L - 1):
             regroup(l, 0, False, 0, F)
@@ -332,11 +332,11 @@ def tile_residualblock5_pa_kernel(tc, x, k1, b1, gamma1, beta1, mean1, var1, out
         multiply(last, 1, 0, CHUNKS)
         quantise(last, "b", CHUNKS, 2 * CHUNKS)
         multiply(last, 2, 0, CHUNKS)
-        for c in range(CHUNKS):
-            regroup(last, 4, c % 2 == 1, c * P, (c + 1) * P)
-        for c in range(CHUNKS):
-            quantise(last, "c", c, c + 1)
-            multiply(last, 4, c, c + 1)
+        regroup(last, 4, False, 0, 384)
+        regroup(last, 4, True, 384, F)
+        for c in range(0, CHUNKS, 2):
+            quantise(last, "c", c, c + 2)
+            multiply(last, 4, c, c + 2)
         finish(last - 1, 0, CHUNKS, True)
         for c in range(CHUNKS):
             affine(last, c, c % 2 == 0)

@@ -27,7 +27,7 @@ PAIRED = (1, 2, 3, 4, 5, 6)
 X_AFTER = {2: 0, 3: 1}
 LOAD_ORDER = (0, 1, 3, 2, 4)
 X_PIECES = (0, 6, 2, 4)
-TAP4_V = (416, 416, 416, 416, 416, 416, 416, 416)
+TAP4_V = (448, 448, 448, 448, 448, 448, 448, 448)
 HOLD = 5
 RUN = 8
 GROUP_OF = {0: ("a", 0), 3: ("a", 1), 1: ("b", 0), 2: ("b", 1), 4: ("c", 0)}

from contextlib import ExitStack

import concourse.mybir as mybir
from concourse.masks import make_identity

F32 = mybir.dt.float32
BF16 = mybir.dt.bfloat16
U32 = mybir.dt.uint32
U8 = mybir.dt.uint8
FP8X4 = mybir.dt.float8_e4m3fn_x4
ALU = mybir.AluOpType
ACT = mybir.ActivationFunctionType

P = 128
PACK = 4
B, L, C, TAPS = 128, 8, 512, 5
F = C
CHUNKS = F // P
STEP = (0, 0, 1, -1, 2)
BN_EPS = 1e-3
ALPHA = 0.3
NM = L * TAPS
FLOPS = 2 * B * L * TAPS * C * F

RAW_BUFS = 8
PAIRED = (1, 2, 3, 4, 5, 6)
X_AFTER = {2: 0, 3: 1}
LOAD_ORDER = (0, 1, 3, 2, 4)
X_PIECES = (0, 6, 2, 4)
TAP4_V = (448, 448, 448, 448, 448, 448, 448, 448)
HOLD = 5
RUN = 8
GROUP_OF = {0: ("a", 0), 3: ("a", 1), 1: ("b", 0), 2: ("b", 1), 4: ("c", 0)}
GROUP_SIZE = {"a": 2, "b": 2, "c": 1}
SUM_ON_PE = True


def tile_residualblock5_pa_kernel(tc, x, k1, b1, gamma1, beta1, mean1, var1, out):
    nc = tc.nc
    with ExitStack() as ctx:
        const = ctx.enter_context(tc.tile_pool(name="const", bufs=1))
        rawp = ctx.enter_context(tc.tile_pool(name="rawp", bufs=RAW_BUFS))
        grpp = ctx.enter_context(tc.tile_pool(name="grpp", bufs=2))
        codep = ctx.enter_context(tc.tile_pool(name="codep", bufs=3))
        epip = ctx.enter_context(tc.tile_pool(name="epip", bufs=3))
        psa = ctx.enter_context(tc.psum_pool(name="psa", bufs=1))
        psm = ctx.enter_context(tc.psum_pool(name="psm", bufs=4))

        seq = []
        for l in range(L):
            if l in PAIRED:
                seq.extend([(l, (0, 1)), (l, (2, 3)), (l, (4,))])
            else:
                seq.extend([(l, (i,)) for i in LOAD_ORDER])
        state = {"next": 0}
        held = {"raw": [], "raw2": []}
        done = set()
        raws, grps, codes, accs, vs, lvs, trs = {}, {}, {}, {}, {}, {}, {}
        x_raw, x_ps, x_grp, zps = {}, {}, {}, {}

        def load_more(l_done, i_done):
            done.add((l_done, i_done))
            while state["next"] < len(seq):
                n = state["next"]
                l, taps = seq[n]
                tag = "raw" if len(taps) == 1 else "raw2"
                k = len(held[tag])
                if k >= RAW_BUFS and not all(m in done for m in held[tag][k - RAW_BUFS]):
                    return
                held[tag].append([(l, i) for i in taps])
                if len(taps) == 1:
                    raw = rawp.tile([P, PACK, F], BF16, name="raw", tag="raw", align_bytes=256)
                    src = k1[taps[0], l, :, :].rearrange("(p j) f -> p j f", j=PACK)
                    nc.sync.dma_start(out=raw[:], in_=src)
                    raws[(l, taps[0])] = raw[:]
                else:
                    raw2 = rawp.tile([P, 2, PACK, F], BF16, name="raw2", tag="raw2", align_bytes=256)
                    nc.sync.dma_start(out=raw2[:].rearrange("p i j f -> p i (j f)"),
                                      in_=k1[taps[0]:taps[1] + 1, l, :, :].rearrange("i (p j) f -> p i (j f)", j=PACK))
                    raws[(l, taps[0])] = raw2[:, 0, :, :]
                    raws[(l, taps[1])] = raw2[:, 1, :, :]
                state["next"] = n + 1
                if n in X_AFTER:
                    load_x(X_AFTER[n])

        def load_x(h):
            xr = const.tile([P, 4 * C], BF16, name="xr%d" % h, align_bytes=256)
            nc.sync.dma_start(out=xr[:], in_=x[:, 4 * h:4 * h + 4, :].rearrange("b l c -> b (l c)"))
            for g, pa in enumerate(X_PIECES):
                if pa // 4 == h:
                    x_raw[g] = xr[:, (pa % 4) * C:(pa % 4 + 2) * C]

        vecs = const.tile([P, F], BF16, name="vecs")
        nc.gpsimd.memset(vecs[:], 0.0)
        warm = const.tile([P, 1], F32, name="warm")
        warm2 = const.tile([P, 1], F32, name="warm2")
        nc.gpsimd.memset(warm[:], 1.0)
        nc.scalar.dma_start(out=vecs[0:L, :], in_=b1)
        for r, vec in enumerate((gamma1, beta1, mean1, var1)):
            nc.scalar.dma_start(out=vecs[L + r:L + r + 1, :], in_=vec.rearrange("(o f) -> o f", o=1))
        nc.scalar.activation(out=warm2[:], in_=warm[:], func=ACT.Abs_reciprocal_sqrt)
        ident_f = const.tile([P, P], F32, name="ident_f")
        make_identity(nc, ident_f[:])
        ident_b = const.tile([P, P], BF16, name="ident_b")
        make_identity(nc, ident_b[:])

        load_more(-1, -1)

        o_all = const.tile([P, L, F], F32, name="o_all", align_bytes=256)
        xq = const.tile([P, L * B], U32, name="xq", align_bytes=64)
        xs = const.tile([P, L * B], U8, name="xs", align_bytes=64)
        s_t = const.tile([P, CHUNKS], F32, name="s_t")
        t_t = const.tile([P, L, CHUNKS], F32, name="t_t")
        vt = const.tile([P, L + 4, CHUNKS], F32, name="vt")
        rs = const.tile([P, CHUNKS], F32, name="rs")
        eps = const.tile([P, 1], F32, name="eps")
        nc.gpsimd.tensor_scalar(out=eps[:], in0=warm[:], scalar1=BN_EPS, scalar2=None, op0=ALU.mult)

        def x_turn(g):
            xv = x_raw[g].bitcast(F32).rearrange("b (l p u) -> b l u p", l=2, u=2)
            xt = psm.tile([P, 4, P], F32, name="xt", tag="m")
            for dl in range(2):
                for u in range(2):
                    nc.tensor.transpose(out=xt[:, 2 * dl + u, :], in_=xv[:, dl, u, :], identity=ident_f[:])
            x_ps[g] = xt

        def x_exit(g):
            gx = const.tile([P, 2 * B * PACK], BF16, name="gx%d" % g, align_bytes=64)
            dst = gx[:].bitcast(F32).rearrange("p (l b u) -> p l b u", l=2, u=2)
            src = x_ps[g][:].rearrange("p (l u) b -> p l b u", u=2)
            nc.scalar.copy(out=dst, in_=src)
            x_grp[g] = gx

        def x_quant(g):
            cols = slice(X_PIECES[g] * B, (X_PIECES[g] + 2) * B)
            nc.vector.quantize_mx(out=xq[:, cols].bitcast(FP8X4), scales=xs[:, cols], in_=x_grp[g][:])

        def bn_part1():
            vps = psm.tile([P, CHUNKS, P], BF16, name="vps", tag="m")
            for c in range(CHUNKS):
                nc.tensor.transpose(out=vps[:, c, :], in_=vecs[:, c * P:(c + 1) * P], identity=ident_b[:])
            nc.vector.tensor_copy(out=vt[:], in_=vps[:, :, 0:L + 4].rearrange("p c r -> p r c"))

        def bn_part2():
            pre = ALPHA if SUM_ON_PE else 1.0
            wide = [P, L, CHUNKS]
            nc.vector.scalar_tensor_tensor(out=s_t[:], in0=vt[:, L, :], scalar=pre, in1=rs[:], op0=ALU.mult, op1=ALU.mult)
            u1 = const.tile(wide, F32, name="u1")
            nc.vector.scalar_tensor_tensor(out=u1[:], in0=vt[:, 0:L, :], scalar=2.0, in1=vt[:, L + 2:L + 3, :].to_broadcast(wide),
                                           op0=ALU.mult, op1=ALU.subtract)
            u2 = const.tile(wide, F32, name="u2")
            nc.vector.tensor_tensor(out=u2[:], in0=u1[:], in1=s_t[:].unsqueeze(1).to_broadcast(wide), op=ALU.mult)
            nc.vector.scalar_tensor_tensor(out=t_t[:], in0=vt[:, L + 1:L + 2, :].to_broadcast(wide), scalar=pre, in1=u2[:],
                                           op0=ALU.mult, op1=ALU.add)

        def regroup(l, i, use_scalar, f0, f1):
            g, place = GROUP_OF[i]
            if (l, g) not in grps:
                grps[(l, g)] = grpp.tile([P, GROUP_SIZE[g], F, PACK], BF16, name="grp" + g, tag="grp" + g, align_bytes=64)
            dst = grps[(l, g)][:, place, f0:f1, :].rearrange("p (c i) t -> p c t i", i=RUN)
            src = raws[(l, i)][:, :, f0:f1].rearrange("p t (c i) -> p c t i", i=RUN)
            if use_scalar:
                nc.scalar.copy(out=dst, in_=src)
            else:
                nc.vector.tensor_copy(out=dst, in_=src)

        def pe_zip(l, i, h):
            half = F // 2
            zp = psm.tile([P, 2, half, 2], BF16, name="zp", tag="m")
            zps[(l, i)] = zp
            for u in range(2):
                nc.tensor.matmul(out=zp[:, u, :, :].rearrange("p f e -> p (f e)"), lhsT=ident_b[:],
                                 rhs=raws[(l, i)][:, 2 * u:2 * u + 2, h * half:(h + 1) * half].rearrange("p e f -> p f e"),
                                 start=True, stop=True)

        def zip_exit(l, i, h):
            g, place = GROUP_OF[i]
            if (l, g) not in grps:
                grps[(l, g)] = grpp.tile([P, GROUP_SIZE[g], F, PACK], BF16, name="grp" + g, tag="grp" + g, align_bytes=64)
            half = F // 2
            zp = zps[(l, i)]
            dst = grps[(l, g)][:, place, h * half:(h + 1) * half, :].rearrange("p f t -> p (f t)").bitcast(F32)
            src = zp[:].rearrange("p u f e -> p (u f e)").bitcast(F32).rearrange("p (u f) -> p f u", u=2)
            nc.scalar.copy(out=dst.rearrange("p (f u) -> p f u", u=2), in_=src)

        def quantise(l, g, c0, c1):
            if (l, g) not in codes:
                wq = codep.tile([P, GROUP_SIZE[g] * F], U32, name="wq" + g, tag="wq" + g, align_bytes=64)
                ws = codep.tile([P, GROUP_SIZE[g] * F], U8, name="ws" + g, tag="ws" + g, align_bytes=64)
                codes[(l, g)] = (wq, ws)
            wq, ws = codes[(l, g)]
            cols = slice(c0 * P, c1 * P)
            nc.vector.quantize_mx(out=wq[:, cols].bitcast(FP8X4), scales=ws[:, cols],
                                  in_=grps[(l, g)][:].rearrange("p n f t -> p (n f) t")[:, cols, :].rearrange("p f t -> p (f t)"))

        def multiply(l, i, c0, c1):
            first = i == 0
            if first:
                accs[l] = [psa.tile([P, B], F32, name="acc%d" % c, tag="acc%d" % c) for c in range(CHUNKS)]
            g, place = GROUP_OF[i]
            wq, ws = codes[(l, g)]
            pos = (l - STEP[i]) % L
            for c in range(c0, c1):
                cols = slice(place * F + c * P, place * F + (c + 1) * P)
                nc.tensor.matmul_mx(
                    out=accs[l][c][:],
                    lhsT=wq[:, cols].bitcast(FP8X4),
                    lhsT_scale=ws[:, cols],
                    rhs=xq[:, pos * B:(pos + 1) * B].bitcast(FP8X4),
                    rhs_scale=xs[:, pos * B:(pos + 1) * B],
                    start=first, stop=(i == TAPS - 1))

        def affine(l, c, use_scalar):
            if l not in vs:
                vs[l] = epip.tile([P, CHUNKS * B], F32, name="v", tag="v")
            if use_scalar:
                nc.scalar.activation(out=vs[l][:, c * B:(c + 1) * B], in_=accs[l][c][:], func=ACT.Identity,
                                     bias=t_t[:, l, c:c + 1], scale=s_t[:, c:c + 1])
            else:
                nc.vector.tensor_scalar(out=vs[l][:, c * B:(c + 1) * B], in0=accs[l][c][:],
                                        scalar1=s_t[:, c:c + 1], scalar2=t_t[:, l, c:c + 1],
                                        op0=ALU.mult, op1=ALU.add)

        def leaky(l, c0, c1, use_scalar):
            if l not in lvs:
                lvs[l] = epip.tile([P, CHUNKS * B], F32, name="lv", tag="lv")
            cols = slice(c0 * B, c1 * B)
            if not SUM_ON_PE:
                nc.vector.scalar_tensor_tensor(out=lvs[l][:, cols], in0=vs[l][:, cols], scalar=ALPHA, in1=vs[l][:, cols],
                                               op0=ALU.mult, op1=ALU.max)
            elif use_scalar:
                nc.scalar.activation(out=lvs[l][:, cols], in_=vs[l][:, cols], func=ACT.Relu, scale=(1.0 - ALPHA) / ALPHA)
            else:
                nc.vector.tensor_scalar(out=lvs[l][:, cols], in0=vs[l][:, cols], scalar1=(1.0 - ALPHA) / ALPHA, scalar2=0.0,
                                        op0=ALU.mult, op1=ALU.max)

        def turn(l, c0, c1):
            tr = psm.tile([P, (c1 - c0) * P], F32, name="tr", tag="m")
            for c in range(c0, c1):
                dst = tr[:, (c - c0) * P:(c - c0 + 1) * P]
                if SUM_ON_PE:
                    nc.tensor.matmul(out=dst, lhsT=vs[l][:, c * B:(c + 1) * B], rhs=ident_f[:], is_transpose=True, start=True, stop=False)
                    nc.tensor.matmul(out=dst, lhsT=lvs[l][:, c * B:(c + 1) * B], rhs=ident_f[:], is_transpose=True, start=False, stop=True)
                else:
                    nc.tensor.transpose(out=dst, in_=lvs[l][:, c * B:(c + 1) * B], identity=ident_f[:])
            trs[(l, c0)] = tr

        def finish(l, c0, c1, use_scalar):
            dst = o_all[:, l, c0 * P:c1 * P]
            if use_scalar:
                nc.scalar.copy(out=dst, in_=trs[(l, c0)][:])
            else:
                nc.vector.tensor_copy(out=dst, in_=trs[(l, c0)][:])
            if l == HOLD - 1:
                nc.sync.dma_start(out=out[:, 0:HOLD, :], in_=o_all[:, 0:HOLD, :])
            elif HOLD <= l < L - 1:
                nc.sync.dma_start(out=out[:, l, :], in_=o_all[:, l, :])

        for l in range(L - 1):
            regroup(l, 0, False, 0, F)
            load_more(l, 0)
            regroup(l, 1, True, 0, F)
            load_more(l, 1)
            regroup(l, 3, False, 0, F)
            load_more(l, 3)
            if l >= 1:
                quantise(l - 1, "c", 0, CHUNKS)
                multiply(l - 1, 4, 0, CHUNKS)
            if l >= 2:
                finish(l - 2, 0, CHUNKS, True)
            if l == 0:
                bn_part1()
                x_turn(0)
                x_exit(0)
                nc.scalar.activation(out=rs[:], in_=vt[:, L + 3, :], func=ACT.Abs_reciprocal_sqrt, bias=eps[:])
            elif l <= 2:
                x_turn(l + 1)
                x_exit(l + 1)
            if l == 0:
                pe_zip(0, 2, 1)
            zip_exit(l, 2, 1)
            if l + 1 < L:
                pe_zip(l + 1, 2, 1)
            regroup(l, 2, True, 0, F // 2)
            load_more(l, 2)
            if l >= 1:
                for c in range(CHUNKS):
                    affine(l - 1, c, True)
                if SUM_ON_PE:
                    leaky(l - 1, 0, CHUNKS, True)
                    turn(l - 1, 0, CHUNKS)
            quantise(l, "a", 0, 2 * CHUNKS)
            if l <= 2:
                x_quant(0 if l == 0 else l + 1)
            multiply(l, 0, 0, CHUNKS)
            multiply(l, 3, 0, CHUNKS)
            if l == 0:
                bn_part2()
                x_turn(1)
                x_exit(1)
            if TAP4_V[l] < F:
                regroup(l, 4, True, TAP4_V[l], F)
            if TAP4_V[l] > 0:
                regroup(l, 4, False, 0, TAP4_V[l])
            load_more(l, 4)
            quantise(l, "b", 0, 2 * CHUNKS)
            if l == 0:
                x_quant(1)
            multiply(l, 1, 0, CHUNKS)
            multiply(l, 2, 0, CHUNKS)
            if l >= 1 and not SUM_ON_PE:
                leaky(l - 1, 0, CHUNKS, False)
                turn(l - 1, 0, CHUNKS)

        last = L - 1
        regroup(last, 0, False, 0, F)
        regroup(last, 1, True, 0, F)
        regroup(last, 3, False, 0, F)
        quantise(last - 1, "c", 0, CHUNKS)
        multiply(last - 1, 4, 0, CHUNKS)
        finish(last - 2, 0, CHUNKS, True)
        zip_exit(last, 2, 1)
        regroup(last, 2, False, 0, F // 2)
        for c in range(CHUNKS):
            affine(last - 1, c, True)
        leaky(last - 1, 0, CHUNKS, True)
        turn(last - 1, 0, CHUNKS)
        quantise(last, "a", 0, 2 * CHUNKS)
        multiply(last, 0, 0, CHUNKS)
        multiply(last, 3, 0, CHUNKS)
        quantise(last, "b", 0, CHUNKS)
        multiply(last, 1, 0, CHUNKS)
        quantise(last, "b", CHUNKS, 2 * CHUNKS)
        multiply(last, 2, 0, CHUNKS)
        regroup(last, 4, False, 0, 384)
        regroup(last, 4, True, 384, F)
        for c in range(0, CHUNKS, 2):
            quantise(last, "c", c, c + 2)
            multiply(last, 4, c, c + 2)
        finish(last - 1, 0, CHUNKS, True)
        for c in range(CHUNKS):
            affine(last, c, c % 2 == 0)
            leaky(last, c, c + 1, c % 2 == 0)
            turn(last, c, c + 1)
        for c in range(CHUNKS):
            finish(last, c, c + 1, c % 2 == 0)
        nc.sync.dma_start(out=out[:, last, :], in_=o_all[:, last, :])
